import numpy as np
import ml_dtypes


def mxq(x, axis, fmt="e4m3"):
    dtype, down = {"e4m3": (ml_dtypes.float8_e4m3fn, 7), "e5m2": (ml_dtypes.float8_e5m2, 14)}[fmt]
    v = np.moveaxis(np.asarray(x, np.float32).astype(ml_dtypes.bfloat16).astype(np.float64), axis, -1)
    blocks = v.reshape(v.shape[:-1] + (-1, 32))
    amax = np.abs(blocks).max(-1, keepdims=True)
    byte = np.maximum(np.where(amax > 0, np.frexp(amax)[1] - 1 + 127, 0) - down, 1)
    scale = np.exp2(byte - 127.0)
    codes = (blocks / scale).astype(np.float32).astype(dtype).astype(np.float64)
    return np.moveaxis((codes * scale).reshape(v.shape), -1, axis)


WIDE = False


def mx_kscale(k):
    if not WIDE:
        return np.ones(k)
    levels = np.array([10, -10, 5, -5, 0])
    a = np.random.permutation(np.resize(levels, k // 512 * 4)).reshape(k // 512, 4)
    idx = np.arange(k)
    return np.exp2(a[idx // 512, idx % 128 // 32])


BF16 = ml_dtypes.bfloat16


def bf(x):
    return np.asarray(x, np.float32).astype(BF16)


def f64(x):
    return np.asarray(x).astype(np.float64)


E2M1 = np.array([0.0, 0.5, 1.0, 1.5, 2.0, 3.0, 4.0, 6.0, -0.0, -0.5, -1.0, -1.5, -2.0, -3.0, -4.0, -6.0])


def pack_weight(w, fmt):
    k, n = w.shape
    w = f64(bf(w)).reshape(k // 32, 32, n)
    amax = np.abs(w).max(1)
    if fmt == "e4m3":
        byte = np.frexp(amax)[1] - 1 + 127 - 7
    else:
        mant, ex = np.frexp(amax / 6.0)
        byte = np.where(mant > 0.5, ex, ex - 1) + 127
    byte = np.clip(np.where(amax > 0, byte, 1), 1, 254)
    scaled = (w * np.exp2(127.0 - byte)[:, None, :]).reshape(k, n).astype(np.float32)
    by_word = np.ascontiguousarray(scaled.reshape(k // 512, 128, 4, n).transpose(0, 1, 3, 2))
    if fmt == "e4m3":
        words = by_word.astype(ml_dtypes.float8_e4m3fn).view(np.uint8)
    else:
        c = by_word.astype(ml_dtypes.float4_e2m1fn).view(np.uint8) & 0xF
        words = c[..., 0::2] | (c[..., 1::2] << 4)
    return np.ascontiguousarray(words), np.ascontiguousarray(byte.astype(np.uint8).reshape(k // 512, 16, n))


def unpack_weight(words, scales, fmt):
    g, p, n, _ = words.shape
    if fmt == "e4m3":
        vals = np.ascontiguousarray(words).view(ml_dtypes.float8_e4m3fn).astype(np.float64)
    else:
        nib = np.empty((g, p, n, 4), np.uint8)
        nib[..., 0::2] = words & 0xF
        nib[..., 1::2] = words >> 4
        vals = E2M1[nib]
    vals = vals * np.repeat(np.exp2(scales.astype(np.float64) - 127.0), 8, axis=1)[..., None]
    return vals.transpose(0, 1, 3, 2).reshape(g * 512, n)


H, I, B = 1024, 1024, 512
FMT = "e4m3"


def sigmoid(v):
    return 1.0 / (1.0 + np.exp(-v))


def log_sigmoid(v):
    return np.minimum(v, 0.0) - np.log(1.0 + np.exp(-np.abs(v)))


def setup_inputs():
    s, t = mx_kscale(I), mx_kscale(H)

    def w():
        return pack_weight(np.ascontiguousarray((np.random.standard_normal((H, I)) * 0.7 / np.sqrt(I) / s).T), FMT)

    def r():
        return pack_weight(np.ascontiguousarray((np.random.standard_normal((H, H)) * 0.7 / np.sqrt(H) / t).T), FMT)

    def b():
        return bf(np.random.standard_normal(H) * 0.3)

    out = {"x": bf(np.random.standard_normal((I, B)) * s[:, None]),
           "h_prev": bf(np.random.standard_normal((H, B)) * t[:, None]),
           "c_prev": bf(np.random.standard_normal((H, B))),
           "n_prev": bf(np.random.uniform(size=(H, B))),
           "m_prev": bf(np.random.standard_normal((H, B)))}
    for gate in ("input", "forget", "output", "z"):
        out["w_" + gate + "_words"], out["w_" + gate + "_scales"] = w()
    for gate in ("input", "forget", "output", "z"):
        out["r_" + gate + "_words"], out["r_" + gate + "_scales"] = r()
    for gate in ("input", "forget", "output", "z"):
        out["b_" + gate] = b()
    return out


def reference(x, h_prev, c_prev, n_prev, m_prev,
              w_input_words, w_input_scales, w_forget_words, w_forget_scales,
              w_output_words, w_output_scales, w_z_words, w_z_scales,
              r_input_words, r_input_scales, r_forget_words, r_forget_scales,
              r_output_words, r_output_scales, r_z_words, r_z_scales,
              b_input, b_forget, b_output, b_z):
    xq = mxq(f64(x), 0, "e4m3")
    hq = mxq(f64(h_prev), 0, "e4m3")
    input_wave = (unpack_weight(w_input_words, w_input_scales, FMT).T @ xq) + (unpack_weight(r_input_words, r_input_scales, FMT).T @ hq) + f64(b_input)[:, None]
    forget_wave = (unpack_weight(w_forget_words, w_forget_scales, FMT).T @ xq) + (unpack_weight(r_forget_words, r_forget_scales, FMT).T @ hq) + f64(b_forget)[:, None]
    output_wave = (unpack_weight(w_output_words, w_output_scales, FMT).T @ xq) + (unpack_weight(r_output_words, r_output_scales, FMT).T @ hq) + f64(b_output)[:, None]
    z_wave = (unpack_weight(w_z_words, w_z_scales, FMT).T @ xq) + (unpack_weight(r_z_words, r_z_scales, FMT).T @ hq) + f64(b_z)[:, None]

    log_i = input_wave
    log_f = log_sigmoid(forget_wave)
    m_t = np.maximum(log_f + f64(m_prev), log_i)
    input_prime = np.exp(log_i - m_t)
    forget_prime = np.exp(log_f + f64(m_prev) - m_t)

    c_t = forget_prime * f64(c_prev) + input_prime * np.tanh(z_wave)
    n_t = forget_prime * f64(n_prev) + forget_prime
    h_wave = c_t / n_t
    h_t = sigmoid(output_wave) * np.tanh(h_wave)
    return (h_t, c_t, n_t, m_t)

@@ -1,0 +1,301 @@
+from contextlib import ExitStack
+
+import concourse.mybir as mybir
+from concourse.masks import make_identity
+
+F32 = mybir.dt.float32
+BF16 = mybir.dt.bfloat16
+I32 = mybir.dt.int32
+U32 = mybir.dt.uint32
+U8 = mybir.dt.uint8
+FP8X4 = mybir.dt.float8_e4m3fn_x4
+FUNC = mybir.ActivationFunctionType
+ALU = mybir.AluOpType
+
+P = 128
+FEATURES = 1024
+BATCH = 512
+TILES = FEATURES // P
+PACK = 4
+K_PASS = P * PACK
+HALVES = FEATURES // K_PASS
+PASSES = 2 * HALVES
+PLANE_ROWS = 4
+QUADRANTS = 4
+
+FORGET = 0
+INPUT = 1
+Z = 2
+OUTPUT = 3
+GATES = 4
+
+EXP_CLAMP = 80.0
+
+FLOPS = 2 * 2 * GATES * FEATURES * FEATURES * BATCH
+
+
+def tile_slstmcell_pa_kernel(
+    tc, x, h_prev, c_prev, n_prev, m_prev,
+    w_input_words, w_input_scales, w_forget_words, w_forget_scales,
+    w_output_words, w_output_scales, w_z_words, w_z_scales,
+    r_input_words, r_input_scales, r_forget_words, r_forget_scales,
+    r_output_words, r_output_scales, r_z_words, r_z_scales,
+    b_input, b_forget, b_output, b_z,
+    out_0, out_1, out_2, out_3,
+):
+    nc = tc.nc
+    h_out, c_out, n_out, m_out = out_0, out_1, out_2, out_3
+    dram_words = {
+        FORGET: (w_forget_words, r_forget_words),
+        INPUT: (w_input_words, r_input_words),
+        Z: (w_z_words, r_z_words),
+        OUTPUT: (w_output_words, r_output_words),
+    }
+    dram_scales = {
+        FORGET: (w_forget_scales, r_forget_scales),
+        INPUT: (w_input_scales, r_input_scales),
+        Z: (w_z_scales, r_z_scales),
+        OUTPUT: (w_output_scales, r_output_scales),
+    }
+    dram_bias = {FORGET: b_forget, INPUT: b_input, Z: b_z, OUTPUT: b_output}
+
+    with ExitStack() as ctx:
+        ctx.enter_context(tc.manual_schedule())
+        keep = ctx.enter_context(tc.tile_pool(name="keep", bufs=1))
+        stage = ctx.enter_context(tc.tile_pool(name="stage", bufs=2))
+        full = ctx.enter_context(tc.tile_pool(name="full", bufs=TILES))
+        work = ctx.enter_context(tc.tile_pool(name="work", bufs=3))
+        psum = ctx.enter_context(tc.psum_pool(name="psum", bufs=8))
+
+        words = {}
+        for gate in range(GATES):
+            for operand in range(2):
+                words[(gate, operand)] = keep.tile(
+                    [P, HALVES, FEATURES], U32, name="words_%d_%d" % (gate, operand), align_bytes=64
+                )
+        planes = keep.tile([P, GATES, FEATURES], U8, align_bytes=64)
+        codes = keep.tile([P, PASSES, BATCH], U32, align_bytes=64)
+        code_planes = keep.tile([P, PASSES, BATCH], U8, align_bytes=64)
+        m_sb = keep.tile([P, TILES, BATCH], BF16)
+        n_sb = keep.tile([P, TILES, BATCH], BF16)
+        c_sb = keep.tile([P, TILES, BATCH], BF16)
+        bias_rows = keep.tile([P, P], BF16)
+        identity = keep.tile([P, P], BF16)
+        bias = keep.tile([P, GATES * TILES], F32)
+        half_bias = keep.tile([P, GATES * TILES], F32)
+        minus_bias = keep.tile([P, GATES * TILES], F32)
+
+        def by_tile(dram):
+            return dram.rearrange("(t p) b -> p t b", p=P)
+
+        def load_scales(gate):
+            for operand in range(2):
+                scales = dram_scales[gate][operand]
+                for quadrant in range(QUADRANTS):
+                    first = 32 * quadrant + PLANE_ROWS * HALVES * operand
+                    nc.sync.dma_start(
+                        out=planes[first : first + PLANE_ROWS * HALVES, gate, :].bitcast(I32),
+                        in_=scales[:, PLANE_ROWS * quadrant : PLANE_ROWS * (quadrant + 1), :].bitcast(I32),
+                    )
+
+        def load_words(gate, operand):
+            for half in range(HALVES):
+                nc.sync.dma_start(
+                    out=words[(gate, operand)][:, half, :].bitcast(I32),
+                    in_=dram_words[gate][operand][half].rearrange("p n t -> p (n t)").bitcast(I32),
+                )
+
+        def load_rows(source):
+            raws = []
+            for half in range(HALVES):
+                raw = stage.tile([P, PACK, BATCH], BF16, tag="raw", bufs=PASSES, name="raw")
+                rows = source[half * K_PASS : (half + 1) * K_PASS, :]
+                nc.sync.dma_start(out=raw[:], in_=rows.rearrange("(p j) b -> p j b", j=PACK))
+                raws.append(raw)
+            return raws
+
+        def quantise(raws, first_pass):
+            groupeds = []
+            for raw in raws:
+                grouped = stage.tile([P, BATCH, PACK], BF16, tag="grouped", name="grouped", align_bytes=64)
+                nc.vector.tensor_copy(
+                    out=grouped[:].rearrange("p (c i) j -> p c j i", i=4),
+                    in_=raw[:].rearrange("p j (c i) -> p c j i", i=4),
+                )
+                groupeds.append(grouped)
+            for half in range(HALVES):
+                nc.vector.quantize_mx(
+                    out=codes[:, first_pass + half, :].bitcast(FP8X4),
+                    scales=code_planes[:, first_pass + half, :],
+                    in_=groupeds[half][:].rearrange("p b j -> p (b j)"),
+                )
+
+        def mx_pass(wave, gate, tile_index, k):
+            operand, half = divmod(k, HALVES)
+            cols = slice(tile_index * P, (tile_index + 1) * P)
+            nc.tensor.matmul_mx(
+                out=wave[:],
+                lhsT=words[(gate, operand)][:, half, cols].bitcast(FP8X4),
+                lhsT_scale=planes[PLANE_ROWS * k : P, gate, cols],
+                rhs=codes[:, k, :].bitcast(FP8X4),
+                rhs_scale=code_planes[:, k, :],
+                start=(k == 0),
+                stop=(k == PASSES - 1),
+            )
+
+        def new_wave(gate, tile_index):
+            return psum.tile([P, BATCH], F32, tag="wave", name="wave_%d_%d" % (gate, tile_index))
+
+        def whole_wave(gate, tile_index):
+            wave = new_wave(gate, tile_index)
+            for k in range(PASSES):
+                mx_pass(wave, gate, tile_index, k)
+            return wave
+
+        def column(table, gate, tile_index):
+            return table[:, TILES * gate + tile_index : TILES * gate + tile_index + 1]
+
+        def store(dram, tile_index, result):
+            nc.sync.dma_start(out=dram[tile_index * P : (tile_index + 1) * P, :], in_=result[:])
+
+        nc.vector.memset(planes[:].bitcast(I32), 0)
+        nc.vector.memset(bias_rows[:], 0.0)
+        make_identity(nc, identity[:])
+        for gate in range(GATES):
+            nc.scalar.dma_start(
+                out=bias_rows[TILES * gate : TILES * (gate + 1), :],
+                in_=dram_bias[gate].rearrange("(t p) -> t p", p=P),
+            )
+        x_raws = load_rows(x)
+        load_scales(FORGET)
+        load_words(FORGET, 0)
+        h_raws = load_rows(h_prev)
+        load_words(FORGET, 1)
+        nc.sync.dma_start(out=m_sb[:], in_=by_tile(m_prev))
+        load_scales(INPUT)
+        load_words(INPUT, 0)
+        load_words(INPUT, 1)
+        nc.sync.dma_start(out=n_sb[:], in_=by_tile(n_prev))
+        nc.sync.dma_start(out=c_sb[:], in_=by_tile(c_prev))
+        load_scales(Z)
+        load_words(Z, 0)
+        load_words(Z, 1)
+        load_scales(OUTPUT)
+        load_words(OUTPUT, 0)
+        load_words(OUTPUT, 1)
+
+        quantise(x_raws, 0)
+        bias_columns = psum.tile([P, P], BF16, tag="wave")
+        nc.tensor.transpose(bias_columns[:], bias_rows[:], identity[:])
+        nc.vector.tensor_copy(out=bias[:], in_=bias_columns[:, 0 : GATES * TILES])
+        nc.vector.tensor_scalar_mul(out=half_bias[:], in0=bias[:], scalar1=0.5)
+        nc.vector.tensor_scalar_mul(out=minus_bias[:], in0=bias[:], scalar1=-1.0)
+        quantise(h_raws, HALVES)
+
+        forget_wave = [new_wave(FORGET, t) for t in range(TILES)]
+        for k in range(PASSES):
+            for t in range(TILES):
+                mx_pass(forget_wave[t], FORGET, t, k)
+
+        sig = []
+        lfm = []
+        input_wave = []
+        for t in range(TILES):
+            sig.append(full.tile([P, BATCH], F32, tag="sig", name="sig_%d" % t))
+            lfm.append(full.tile([P, BATCH], F32, tag="lfm", name="lfm_%d" % t))
+            nc.scalar.activation(
+                out=sig[t][:], in_=forget_wave[t][:], func=FUNC.Tanh,
+                bias=column(half_bias, FORGET, t), scale=0.5,
+            )
+            nc.vector.scalar_tensor_tensor(
+                out=sig[t][:], in0=sig[t][:], scalar=-1.0, in1=sig[t][:], op0=ALU.mult, op1=ALU.max
+            )
+            nc.vector.scalar_tensor_tensor(
+                out=lfm[t][:], in0=forget_wave[t][:], scalar=column(minus_bias, FORGET, t),
+                in1=m_sb[:, t, :], op0=ALU.min, op1=ALU.add,
+            )
+            input_wave.append(whole_wave(INPUT, t))
+
+        for t in range(TILES):
+            nc.scalar.activation(out=sig[t][:], in_=sig[t][:], func=FUNC.Ln, bias=0.5, scale=0.5)
+        ln_n1 = []
+        for t in range(TILES):
+            ln_n1.append(full.tile([P, BATCH], F32, tag="ln_n1", name="ln_n1_%d" % t))
+            nc.scalar.activation(out=ln_n1[t][:], in_=n_sb[:, t, :], func=FUNC.Ln, bias=1.0, scale=1.0)
+
+        z_wave = []
+        for t in range(TILES):
+            nc.vector.scalar_tensor_tensor(
+                out=lfm[t][:], in0=lfm[t][:], scalar=column(bias, FORGET, t), in1=sig[t][:],
+                op0=ALU.add, op1=ALU.add,
+            )
+            m_t = work.tile([P, BATCH], F32, tag="m_t", bufs=5)
+            nc.vector.scalar_tensor_tensor(
+                out=m_t[:], in0=input_wave[t][:], scalar=column(bias, INPUT, t), in1=lfm[t][:],
+                op0=ALU.add, op1=ALU.max,
+            )
+            store(m_out, t, m_t)
+            nc.vector.scalar_tensor_tensor(
+                out=sig[t][:], in0=input_wave[t][:], scalar=column(bias, INPUT, t), in1=lfm[t][:],
+                op0=ALU.add, op1=ALU.subtract,
+            )
+            nc.vector.scalar_tensor_tensor(
+                out=sig[t][:], in0=sig[t][:], scalar=EXP_CLAMP, in1=ln_n1[t][:],
+                op0=ALU.min, op1=ALU.subtract,
+            )
+            z_wave.append(whole_wave(Z, t))
+
+        c_over_n1 = []
+        for t in range(TILES):
+            c_over_n1.append(full.tile([P, BATCH], F32, tag="c_over_n1", name="c_over_n1_%d" % t))
+            nc.scalar.activation(out=c_over_n1[t][:], in_=ln_n1[t][:], func=FUNC.Exp, scale=-1.0)
+            nc.gpsimd.tensor_tensor(
+                out=c_over_n1[t][:], in0=c_over_n1[t][:], in1=c_sb[:, t, :], op=ALU.mult
+            )
+
+        exp_g = []
+        exp_minus_g = []
+        ratio = []
+        output_wave = []
+        for t in range(TILES):
+            exp_g.append(full.tile([P, BATCH], F32, tag="lfm", name="exp_g_%d" % t))
+            exp_minus_g.append(full.tile([P, BATCH], F32, tag="ln_n1", name="exp_minus_g_%d" % t))
+            nc.scalar.activation(out=exp_g[t][:], in_=sig[t][:], func=FUNC.Exp)
+            nc.scalar.activation(out=exp_minus_g[t][:], in_=sig[t][:], func=FUNC.Exp, scale=-1.0)
+            ratio.append(full.tile([P, BATCH], F32, tag="sig", name="ratio_%d" % t))
+            nc.scalar.activation(
+                out=ratio[t][:], in_=z_wave[t][:], func=FUNC.Tanh, bias=column(bias, Z, t)
+            )
+            output_wave.append(whole_wave(OUTPUT, t))
+
+        def last_product(tile_index, tanh_ratio, gate_o):
+            nc.vector.tensor_tensor(out=tanh_ratio[:], in0=tanh_ratio[:], in1=gate_o[:], op=ALU.mult)
+            store(h_out, tile_index, tanh_ratio)
+
+        waiting = None
+        for t in range(TILES):
+            gate_o = work.tile([P, BATCH], F32, tag="gate_o")
+            nc.scalar.activation(
+                out=gate_o[:], in_=output_wave[t][:], func=FUNC.Tanh,
+                bias=column(half_bias, OUTPUT, t), scale=0.5,
+            )
+            nc.gpsimd.tensor_scalar(
+                out=gate_o[:], in0=gate_o[:], scalar1=0.5, scalar2=0.5, op0=ALU.mult, op1=ALU.add
+            )
+            n_t = work.tile([P, BATCH], F32, tag="n_t")
+            nc.vector.scalar_tensor_tensor(
+                out=n_t[:], in0=n_sb[:, t, :], scalar=1.0, in1=exp_minus_g[t][:],
+                op0=ALU.add, op1=ALU.min,
+            )
+            store(n_out, t, n_t)
+            nc.vector.tensor_tensor(out=ratio[t][:], in0=ratio[t][:], in1=exp_g[t][:], op=ALU.mult)
+            nc.vector.tensor_tensor(out=ratio[t][:], in0=ratio[t][:], in1=c_over_n1[t][:], op=ALU.add)
+            tanh_ratio = work.tile([P, BATCH], F32, tag="tanh_ratio")
+            nc.scalar.activation(out=tanh_ratio[:], in_=ratio[t][:], func=FUNC.Tanh)
+            c_t = work.tile([P, BATCH], F32, tag="c_t")
+            nc.vector.tensor_tensor(out=c_t[:], in0=n_t[:], in1=ratio[t][:], op=ALU.mult)
+            store(c_out, t, c_t)
+            if waiting is not None:
+                last_product(*waiting)
+            waiting = (t, tanh_ratio, gate_o)
+        last_product(*waiting)

@@ -65,7 +65,7 @@ def tile_slstmcell_pa_kernel(
         stage = ctx.enter_context(tc.tile_pool(name="stage", bufs=2))
         full = ctx.enter_context(tc.tile_pool(name="full", bufs=TILES))
         work = ctx.enter_context(tc.tile_pool(name="work", bufs=3))
-        psum = ctx.enter_context(tc.psum_pool(name="psum", bufs=8))
+        psum = ctx.enter_context(tc.psum_pool(name="psum", bufs=1))
 
         words = {}
         for gate in range(GATES):
@@ -73,7 +73,7 @@ def tile_slstmcell_pa_kernel(
                 words[(gate, operand)] = keep.tile(
                     [P, HALVES, FEATURES], U32, name="words_%d_%d" % (gate, operand), align_bytes=64
                 )
-        planes = keep.tile([P, GATES, FEATURES], U8, align_bytes=64)
+        planes = keep.tile([P, GATES, 2, FEATURES], U8, align_bytes=64)
         codes = keep.tile([P, PASSES, BATCH], U32, align_bytes=64)
         code_planes = keep.tile([P, PASSES, BATCH], U8, align_bytes=64)
         m_sb = keep.tile([P, TILES, BATCH], BF16)
@@ -88,21 +88,18 @@ def tile_slstmcell_pa_kernel(
         def by_tile(dram):
             return dram.rearrange("(t p) b -> p t b", p=P)
 
-        def load_scales(gate):
-            for operand in range(2):
-                scales = dram_scales[gate][operand]
-                for quadrant in range(QUADRANTS):
-                    first = 32 * quadrant + PLANE_ROWS * HALVES * operand
-                    nc.sync.dma_start(
-                        out=planes[first : first + PLANE_ROWS * HALVES, gate, :].bitcast(I32),
-                        in_=scales[:, PLANE_ROWS * quadrant : PLANE_ROWS * (quadrant + 1), :].bitcast(I32),
-                    )
-
-        def load_words(gate, operand):
+        def load_weight(gate, operand):
             for half in range(HALVES):
                 nc.sync.dma_start(
                     out=words[(gate, operand)][:, half, :].bitcast(I32),
                     in_=dram_words[gate][operand][half].rearrange("p n t -> p (n t)").bitcast(I32),
+                )
+            scales = dram_scales[gate][operand]
+            for quadrant in range(QUADRANTS):
+                first = 32 * quadrant
+                nc.sync.dma_start(
+                    out=planes[first : first + PLANE_ROWS * HALVES, gate, operand, :].bitcast(I32),
+                    in_=scales[:, PLANE_ROWS * quadrant : PLANE_ROWS * (quadrant + 1), :].bitcast(I32),
                 )
 
         def load_rows(source):
@@ -114,15 +111,20 @@ def tile_slstmcell_pa_kernel(
                 raws.append(raw)
             return raws
 
-        def quantise(raws, first_pass):
+        def regroup(copy, raws):
             groupeds = []
             for raw in raws:
-                grouped = stage.tile([P, BATCH, PACK], BF16, tag="grouped", name="grouped", align_bytes=64)
-                nc.vector.tensor_copy(
+                grouped = stage.tile(
+                    [P, BATCH, PACK], BF16, tag="grouped", bufs=PASSES, name="grouped", align_bytes=64
+                )
+                copy(
                     out=grouped[:].rearrange("p (c i) j -> p c j i", i=4),
                     in_=raw[:].rearrange("p j (c i) -> p c j i", i=4),
                 )
                 groupeds.append(grouped)
+            return groupeds
+
+        def quantise(groupeds, first_pass):
             for half in range(HALVES):
                 nc.vector.quantize_mx(
                     out=codes[:, first_pass + half, :].bitcast(FP8X4),
@@ -136,7 +138,7 @@ def tile_slstmcell_pa_kernel(
             nc.tensor.matmul_mx(
                 out=wave[:],
                 lhsT=words[(gate, operand)][:, half, cols].bitcast(FP8X4),
-                lhsT_scale=planes[PLANE_ROWS * k : P, gate, cols],
+                lhsT_scale=planes[PLANE_ROWS * half : P, gate, operand, cols],
                 rhs=codes[:, k, :].bitcast(FP8X4),
                 rhs_scale=code_planes[:, k, :],
                 start=(k == 0),
@@ -144,7 +146,7 @@ def tile_slstmcell_pa_kernel(
             )
 
         def new_wave(gate, tile_index):
-            return psum.tile([P, BATCH], F32, tag="wave", name="wave_%d_%d" % (gate, tile_index))
+            return psum.tile([P, BATCH], F32, tag="bank_%d" % tile_index, name="wave_%d_%d" % (gate, tile_index))
 
         def whole_wave(gate, tile_index):
             wave = new_wave(gate, tile_index)
@@ -158,6 +160,13 @@ def tile_slstmcell_pa_kernel(
         def store(dram, tile_index, result):
             nc.sync.dma_start(out=dram[tile_index * P : (tile_index + 1) * P, :], in_=result[:])
 
+        def alternate(tiles, *stages):
+            for stage_of in stages:
+                for t in tiles:
+                    stage_of(t)
+
+        pairs = [(t, t + 1) for t in range(0, TILES, 2)]
+
         nc.vector.memset(planes[:].bitcast(I32), 0)
         nc.vector.memset(bias_rows[:], 0.0)
         make_identity(nc, identity[:])
@@ -167,42 +176,43 @@ def tile_slstmcell_pa_kernel(
                 in_=dram_bias[gate].rearrange("(t p) -> t p", p=P),
             )
         x_raws = load_rows(x)
-        load_scales(FORGET)
-        load_words(FORGET, 0)
+        load_weight(FORGET, 0)
         h_raws = load_rows(h_prev)
-        load_words(FORGET, 1)
+        load_weight(FORGET, 1)
         nc.sync.dma_start(out=m_sb[:], in_=by_tile(m_prev))
-        load_scales(INPUT)
-        load_words(INPUT, 0)
-        load_words(INPUT, 1)
+        load_weight(INPUT, 0)
+        load_weight(INPUT, 1)
         nc.sync.dma_start(out=n_sb[:], in_=by_tile(n_prev))
+        load_weight(Z, 0)
+        load_weight(Z, 1)
         nc.sync.dma_start(out=c_sb[:], in_=by_tile(c_prev))
-        load_scales(Z)
-        load_words(Z, 0)
-        load_words(Z, 1)
-        load_scales(OUTPUT)
-        load_words(OUTPUT, 0)
-        load_words(OUTPUT, 1)
+        load_weight(OUTPUT, 0)
+        load_weight(OUTPUT, 1)
 
-        quantise(x_raws, 0)
-        bias_columns = psum.tile([P, P], BF16, tag="wave")
+        bias_columns = psum.tile([P, P], BF16, tag="bank_%d" % (TILES - 1))
         nc.tensor.transpose(bias_columns[:], bias_rows[:], identity[:])
+        quantise(regroup(nc.vector.tensor_copy, x_raws), 0)
         nc.vector.tensor_copy(out=bias[:], in_=bias_columns[:, 0 : GATES * TILES])
         nc.vector.tensor_scalar_mul(out=half_bias[:], in0=bias[:], scalar1=0.5)
         nc.vector.tensor_scalar_mul(out=minus_bias[:], in0=bias[:], scalar1=-1.0)
-        quantise(h_raws, HALVES)
+        quantise(regroup(nc.vector.tensor_copy, h_raws), HALVES)
 
         forget_wave = [new_wave(FORGET, t) for t in range(TILES)]
-        for k in range(PASSES):
+        for k in range(HALVES):
             for t in range(TILES):
                 mx_pass(forget_wave[t], FORGET, t, k)
-
-        sig = []
-        lfm = []
-        input_wave = []
         for t in range(TILES):
-            sig.append(full.tile([P, BATCH], F32, tag="sig", name="sig_%d" % t))
-            lfm.append(full.tile([P, BATCH], F32, tag="lfm", name="lfm_%d" % t))
+            for k in range(HALVES, PASSES):
+                mx_pass(forget_wave[t], FORGET, t, k)
+
+        sig = {}
+        lfm = {}
+        ln_n1 = {}
+        input_wave = {}
+        z_wave = {}
+        output_wave = {}
+        for t in range(TILES):
+            sig[t] = full.tile([P, BATCH], F32, tag="sig", name="sig_%d" % t)
             nc.scalar.activation(
                 out=sig[t][:], in_=forget_wave[t][:], func=FUNC.Tanh,
                 bias=column(half_bias, FORGET, t), scale=0.5,
@@ -210,92 +220,129 @@ def tile_slstmcell_pa_kernel(
             nc.vector.scalar_tensor_tensor(
                 out=sig[t][:], in0=sig[t][:], scalar=-1.0, in1=sig[t][:], op0=ALU.mult, op1=ALU.max
             )
+        for t in range(TILES):
+            lfm[t] = full.tile([P, BATCH], F32, tag="lfm", name="lfm_%d" % t)
             nc.vector.scalar_tensor_tensor(
                 out=lfm[t][:], in0=forget_wave[t][:], scalar=column(minus_bias, FORGET, t),
                 in1=m_sb[:, t, :], op0=ALU.min, op1=ALU.add,
             )
-            input_wave.append(whole_wave(INPUT, t))
+            input_wave[t] = whole_wave(INPUT, t)
 
         for t in range(TILES):
             nc.scalar.activation(out=sig[t][:], in_=sig[t][:], func=FUNC.Ln, bias=0.5, scale=0.5)
-        ln_n1 = []
         for t in range(TILES):
-            ln_n1.append(full.tile([P, BATCH], F32, tag="ln_n1", name="ln_n1_%d" % t))
+            ln_n1[t] = full.tile([P, BATCH], F32, tag="ln_n1", name="ln_n1_%d" % t)
             nc.scalar.activation(out=ln_n1[t][:], in_=n_sb[:, t, :], func=FUNC.Ln, bias=1.0, scale=1.0)
 
-        z_wave = []
-        for t in range(TILES):
+        def add_log_sigmoid(t):
             nc.vector.scalar_tensor_tensor(
                 out=lfm[t][:], in0=lfm[t][:], scalar=column(bias, FORGET, t), in1=sig[t][:],
                 op0=ALU.add, op1=ALU.add,
             )
+
+        def new_stabiliser(t):
             m_t = work.tile([P, BATCH], F32, tag="m_t", bufs=5)
             nc.vector.scalar_tensor_tensor(
                 out=m_t[:], in0=input_wave[t][:], scalar=column(bias, INPUT, t), in1=lfm[t][:],
                 op0=ALU.add, op1=ALU.max,
             )
             store(m_out, t, m_t)
+
+        def difference(t):
             nc.vector.scalar_tensor_tensor(
                 out=sig[t][:], in0=input_wave[t][:], scalar=column(bias, INPUT, t), in1=lfm[t][:],
                 op0=ALU.add, op1=ALU.subtract,
             )
+
+        def exponent(t):
             nc.vector.scalar_tensor_tensor(
                 out=sig[t][:], in0=sig[t][:], scalar=EXP_CLAMP, in1=ln_n1[t][:],
                 op0=ALU.min, op1=ALU.subtract,
             )
-            z_wave.append(whole_wave(Z, t))
 
-        c_over_n1 = []
-        for t in range(TILES):
-            c_over_n1.append(full.tile([P, BATCH], F32, tag="c_over_n1", name="c_over_n1_%d" % t))
+        def z_matmuls(t):
+            z_wave[t] = whole_wave(Z, t)
+
+        exp_g = {}
+        n_t = {}
+        ratio = {}
+        c_over_n1 = {}
+
+        def exp_plus(t):
+            exp_g[t] = full.tile([P, BATCH], F32, tag="lfm", name="exp_g_%d" % t)
+            nc.scalar.activation(out=exp_g[t][:], in_=sig[t][:], func=FUNC.Exp)
+
+        def inverse_n1(t):
+            c_over_n1[t] = full.tile([P, BATCH], F32, tag="c_over_n1", name="c_over_n1_%d" % t)
             nc.scalar.activation(out=c_over_n1[t][:], in_=ln_n1[t][:], func=FUNC.Exp, scale=-1.0)
             nc.gpsimd.tensor_tensor(
                 out=c_over_n1[t][:], in0=c_over_n1[t][:], in1=c_sb[:, t, :], op=ALU.mult
             )
 
-        exp_g = []
-        exp_minus_g = []
-        ratio = []
-        output_wave = []
-        for t in range(TILES):
-            exp_g.append(full.tile([P, BATCH], F32, tag="lfm", name="exp_g_%d" % t))
-            exp_minus_g.append(full.tile([P, BATCH], F32, tag="ln_n1", name="exp_minus_g_%d" % t))
-            nc.scalar.activation(out=exp_g[t][:], in_=sig[t][:], func=FUNC.Exp)
-            nc.scalar.activation(out=exp_minus_g[t][:], in_=sig[t][:], func=FUNC.Exp, scale=-1.0)
-            ratio.append(full.tile([P, BATCH], F32, tag="sig", name="ratio_%d" % t))
+        def exp_minus(t):
+            n_t[t] = full.tile([P, BATCH], F32, tag="ln_n1", name="n_t_%d" % t)
+            nc.scalar.activation(out=n_t[t][:], in_=sig[t][:], func=FUNC.Exp, scale=-1.0)
+
+        def tanh_z(t):
+            ratio[t] = full.tile([P, BATCH], F32, tag="sig", name="ratio_%d" % t)
             nc.scalar.activation(
                 out=ratio[t][:], in_=z_wave[t][:], func=FUNC.Tanh, bias=column(bias, Z, t)
             )
-            output_wave.append(whole_wave(OUTPUT, t))
+            output_wave[t] = whole_wave(OUTPUT, t)
 
-        def last_product(tile_index, tanh_ratio, gate_o):
-            nc.vector.tensor_tensor(out=tanh_ratio[:], in0=tanh_ratio[:], in1=gate_o[:], op=ALU.mult)
-            store(h_out, tile_index, tanh_ratio)
+        gate_o = {}
 
-        waiting = None
-        for t in range(TILES):
-            gate_o = work.tile([P, BATCH], F32, tag="gate_o")
+        def output_gate(t):
+            gate_o[t] = work.tile([P, BATCH], F32, tag="gate_o", bufs=6, name="gate_o_%d" % t)
             nc.scalar.activation(
-                out=gate_o[:], in_=output_wave[t][:], func=FUNC.Tanh,
+                out=gate_o[t][:], in_=output_wave[t][:], func=FUNC.Tanh,
                 bias=column(half_bias, OUTPUT, t), scale=0.5,
             )
             nc.gpsimd.tensor_scalar(
-                out=gate_o[:], in0=gate_o[:], scalar1=0.5, scalar2=0.5, op0=ALU.mult, op1=ALU.add
+                out=gate_o[t][:], in0=gate_o[t][:], scalar1=0.5, scalar2=0.5, op0=ALU.mult, op1=ALU.add
             )
-            n_t = work.tile([P, BATCH], F32, tag="n_t")
+
+        def normaliser(t):
             nc.vector.scalar_tensor_tensor(
-                out=n_t[:], in0=n_sb[:, t, :], scalar=1.0, in1=exp_minus_g[t][:],
-                op0=ALU.add, op1=ALU.min,
+                out=n_t[t][:], in0=n_sb[:, t, :], scalar=1.0, in1=n_t[t][:], op0=ALU.add, op1=ALU.min
             )
-            store(n_out, t, n_t)
+            store(n_out, t, n_t[t])
+
+        def weigh_z(t):
             nc.vector.tensor_tensor(out=ratio[t][:], in0=ratio[t][:], in1=exp_g[t][:], op=ALU.mult)
+
+        def add_c(t):
             nc.vector.tensor_tensor(out=ratio[t][:], in0=ratio[t][:], in1=c_over_n1[t][:], op=ALU.add)
-            tanh_ratio = work.tile([P, BATCH], F32, tag="tanh_ratio")
-            nc.scalar.activation(out=tanh_ratio[:], in_=ratio[t][:], func=FUNC.Tanh)
-            c_t = work.tile([P, BATCH], F32, tag="c_t")
-            nc.vector.tensor_tensor(out=c_t[:], in0=n_t[:], in1=ratio[t][:], op=ALU.mult)
+
+        def tanh_ratio(t):
+            nc.scalar.activation(out=ratio[t][:], in_=ratio[t][:], func=FUNC.Tanh)
+
+        def cell(t):
+            c_t = full.tile([P, BATCH], F32, tag="lfm", name="c_t_%d" % t)
+            nc.vector.tensor_tensor(out=c_t[:], in0=n_t[t][:], in1=ratio[t][:], op=ALU.mult)
             store(c_out, t, c_t)
-            if waiting is not None:
-                last_product(*waiting)
-            waiting = (t, tanh_ratio, gate_o)
-        last_product(*waiting)
+
+        def hidden(t):
+            nc.vector.tensor_tensor(out=ratio[t][:], in0=ratio[t][:], in1=gate_o[t][:], op=ALU.mult)
+            store(h_out, t, ratio[t])
+
+        def stage_1(pair):
+            alternate(pair, add_log_sigmoid, new_stabiliser, difference, exponent, z_matmuls)
+
+        def stage_2(pair):
+            alternate(pair, exp_plus, inverse_n1, exp_minus, tanh_z)
+
+        def stage_3(pair):
+            alternate(pair, output_gate, normaliser, weigh_z, add_c, cell)
+
+        def stage_4(pair):
+            alternate(pair, tanh_ratio)
+
+        def stage_5(pair):
+            alternate(pair, hidden)
+
+        stages = (stage_1, stage_2, stage_3, stage_4, stage_5)
+        for step in range(len(pairs) + len(stages) - 1):
+            for depth, stage_of_pair in enumerate(stages):
+                if 0 <= step - depth < len(pairs):
+                    stage_of_pair(pairs[step - depth])

@@ -95,11 +95,12 @@ def tile_slstmcell_pa_kernel(
                     in_=dram_words[gate][operand][half].rearrange("p n t -> p (n t)").bitcast(I32),
                 )
             scales = dram_scales[gate][operand]
+            queue, word = (nc.sync, I32) if gate == FORGET else (nc.gpsimd, F32)
             for quadrant in range(QUADRANTS):
                 first = 32 * quadrant
-                nc.sync.dma_start(
-                    out=planes[first : first + PLANE_ROWS * HALVES, gate, operand, :].bitcast(I32),
-                    in_=scales[:, PLANE_ROWS * quadrant : PLANE_ROWS * (quadrant + 1), :].bitcast(I32),
+                queue.dma_start(
+                    out=planes[first : first + PLANE_ROWS * HALVES, gate, operand, :].bitcast(word),
+                    in_=scales[:, PLANE_ROWS * quadrant : PLANE_ROWS * (quadrant + 1), :].bitcast(word),
                 )
 
         def load_rows(source):

@@ -276,9 +276,6 @@ def tile_slstmcell_pa_kernel(
         def inverse_n1(t):
             c_over_n1[t] = full.tile([P, BATCH], F32, tag="c_over_n1", name="c_over_n1_%d" % t)
             nc.scalar.activation(out=c_over_n1[t][:], in_=ln_n1[t][:], func=FUNC.Exp, scale=-1.0)
-            nc.gpsimd.tensor_tensor(
-                out=c_over_n1[t][:], in0=c_over_n1[t][:], in1=c_sb[:, t, :], op=ALU.mult
-            )
 
         def exp_minus(t):
             n_t[t] = full.tile([P, BATCH], F32, tag="ln_n1", name="n_t_%d" % t)
@@ -299,8 +296,13 @@ def tile_slstmcell_pa_kernel(
                 out=gate_o[t][:], in_=output_wave[t][:], func=FUNC.Tanh,
                 bias=column(half_bias, OUTPUT, t), scale=0.5,
             )
-            nc.gpsimd.tensor_scalar(
-                out=gate_o[t][:], in0=gate_o[t][:], scalar1=0.5, scalar2=0.5, op0=ALU.mult, op1=ALU.add
+
+        def finish_output_gate(t):
+            nc.scalar.activation(out=gate_o[t][:], in_=gate_o[t][:], func=FUNC.Identity, bias=0.5, scale=0.5)
+
+        def divide_c(t):
+            nc.vector.tensor_tensor(
+                out=c_over_n1[t][:], in0=c_over_n1[t][:], in1=c_sb[:, t, :], op=ALU.mult
             )
 
         def normaliser(t):
@@ -334,7 +336,7 @@ def tile_slstmcell_pa_kernel(
             alternate(pair, exp_plus, inverse_n1, exp_minus, tanh_z)
 
         def stage_3(pair):
-            alternate(pair, output_gate, normaliser, weigh_z, add_c, cell)
+            alternate(pair, output_gate, finish_output_gate, divide_c, normaliser, weigh_z, add_c, cell)
 
         def stage_4(pair):
             alternate(pair, tanh_ratio)

@@ -1,3 +1,4 @@
+import math
 from contextlib import ExitStack
 
 import concourse.mybir as mybir
@@ -81,6 +82,7 @@ def tile_slstmcell_pa_kernel(
         c_sb = keep.tile([P, TILES, BATCH], BF16)
         bias_rows = keep.tile([P, P], BF16)
         identity = keep.tile([P, P], BF16)
+        identity_f32 = keep.tile([P, P], F32)
         bias = keep.tile([P, GATES * TILES], F32)
         half_bias = keep.tile([P, GATES * TILES], F32)
         minus_bias = keep.tile([P, GATES * TILES], F32)
@@ -171,6 +173,7 @@ def tile_slstmcell_pa_kernel(
         nc.vector.memset(planes[:].bitcast(I32), 0)
         nc.vector.memset(bias_rows[:], 0.0)
         make_identity(nc, identity[:])
+        make_identity(nc, identity_f32[:])
         for gate in range(GATES):
             nc.scalar.dma_start(
                 out=bias_rows[TILES * gate : TILES * (gate + 1), :],
@@ -206,146 +209,128 @@ def tile_slstmcell_pa_kernel(
             for k in range(HALVES, PASSES):
                 mx_pass(forget_wave[t], FORGET, t, k)
 
-        sig = {}
-        lfm = {}
-        ln_n1 = {}
-        input_wave = {}
-        z_wave = {}
-        output_wave = {}
+        first = {}
+        second = {}
+        third = {}
+        fourth = {}
+        gate_o = {}
+        wave = {}
         for t in range(TILES):
-            sig[t] = full.tile([P, BATCH], F32, tag="sig", name="sig_%d" % t)
+            first[t] = full.tile([P, BATCH], F32, tag="first", name="first_%d" % t)
             nc.scalar.activation(
-                out=sig[t][:], in_=forget_wave[t][:], func=FUNC.Tanh,
+                out=first[t][:], in_=forget_wave[t][:], func=FUNC.Tanh,
                 bias=column(half_bias, FORGET, t), scale=0.5,
             )
             nc.vector.scalar_tensor_tensor(
-                out=sig[t][:], in0=sig[t][:], scalar=-1.0, in1=sig[t][:], op0=ALU.mult, op1=ALU.max
+                out=first[t][:], in0=first[t][:], scalar=-1.0, in1=first[t][:], op0=ALU.mult, op1=ALU.max
             )
         for t in range(TILES):
-            lfm[t] = full.tile([P, BATCH], F32, tag="lfm", name="lfm_%d" % t)
+            second[t] = full.tile([P, BATCH], F32, tag="second", name="second_%d" % t)
             nc.vector.scalar_tensor_tensor(
-                out=lfm[t][:], in0=forget_wave[t][:], scalar=column(minus_bias, FORGET, t),
+                out=second[t][:], in0=forget_wave[t][:], scalar=column(minus_bias, FORGET, t),
                 in1=m_sb[:, t, :], op0=ALU.min, op1=ALU.add,
             )
-            input_wave[t] = whole_wave(INPUT, t)
+            wave[t] = whole_wave(INPUT, t)
 
         for t in range(TILES):
-            nc.scalar.activation(out=sig[t][:], in_=sig[t][:], func=FUNC.Ln, bias=0.5, scale=0.5)
+            nc.scalar.activation(out=first[t][:], in_=first[t][:], func=FUNC.Ln, bias=0.5, scale=0.5)
         for t in range(TILES):
-            ln_n1[t] = full.tile([P, BATCH], F32, tag="ln_n1", name="ln_n1_%d" % t)
-            nc.scalar.activation(out=ln_n1[t][:], in_=n_sb[:, t, :], func=FUNC.Ln, bias=1.0, scale=1.0)
+            third[t] = full.tile([P, BATCH], F32, tag="third", name="third_%d" % t)
+            nc.scalar.activation(out=third[t][:], in_=n_sb[:, t, :], func=FUNC.Ln, bias=1.0, scale=1.0)
 
         def add_log_sigmoid(t):
             nc.vector.scalar_tensor_tensor(
-                out=lfm[t][:], in0=lfm[t][:], scalar=column(bias, FORGET, t), in1=sig[t][:],
+                out=second[t][:], in0=second[t][:], scalar=column(bias, FORGET, t), in1=first[t][:],
                 op0=ALU.add, op1=ALU.add,
             )
 
         def new_stabiliser(t):
             m_t = work.tile([P, BATCH], F32, tag="m_t", bufs=5)
             nc.vector.scalar_tensor_tensor(
-                out=m_t[:], in0=input_wave[t][:], scalar=column(bias, INPUT, t), in1=lfm[t][:],
+                out=m_t[:], in0=wave[t][:], scalar=column(bias, INPUT, t), in1=second[t][:],
                 op0=ALU.add, op1=ALU.max,
             )
             store(m_out, t, m_t)
 
         def difference(t):
             nc.vector.scalar_tensor_tensor(
-                out=sig[t][:], in0=input_wave[t][:], scalar=column(bias, INPUT, t), in1=lfm[t][:],
+                out=first[t][:], in0=wave[t][:], scalar=column(bias, INPUT, t), in1=second[t][:],
                 op0=ALU.add, op1=ALU.subtract,
             )
 
         def exponent(t):
             nc.vector.scalar_tensor_tensor(
-                out=sig[t][:], in0=sig[t][:], scalar=EXP_CLAMP, in1=ln_n1[t][:],
+                out=second[t][:], in0=first[t][:], scalar=EXP_CLAMP, in1=third[t][:],
                 op0=ALU.min, op1=ALU.subtract,
             )
 
         def z_matmuls(t):
-            z_wave[t] = whole_wave(Z, t)
-
-        exp_g = {}
-        n_t = {}
-        ratio = {}
-        c_over_n1 = {}
+            wave[t] = whole_wave(Z, t)
 
         def exp_plus(t):
-            exp_g[t] = full.tile([P, BATCH], F32, tag="lfm", name="exp_g_%d" % t)
-            nc.scalar.activation(out=exp_g[t][:], in_=sig[t][:], func=FUNC.Exp)
-
-        def inverse_n1(t):
-            c_over_n1[t] = full.tile([P, BATCH], F32, tag="c_over_n1", name="c_over_n1_%d" % t)
-            nc.scalar.activation(out=c_over_n1[t][:], in_=ln_n1[t][:], func=FUNC.Exp, scale=-1.0)
+            nc.scalar.activation(out=first[t][:], in_=first[t][:], func=FUNC.Exp)
 
         def exp_minus(t):
-            n_t[t] = full.tile([P, BATCH], F32, tag="ln_n1", name="n_t_%d" % t)
-            nc.scalar.activation(out=n_t[t][:], in_=sig[t][:], func=FUNC.Exp, scale=-1.0)
+            nc.scalar.activation(out=second[t][:], in_=second[t][:], func=FUNC.Exp, scale=-1.0)
+
+        def inverse_n1(t):
+            nc.scalar.activation(out=third[t][:], in_=third[t][:], func=FUNC.Exp, scale=-1.0)
 
         def tanh_z(t):
-            ratio[t] = full.tile([P, BATCH], F32, tag="sig", name="ratio_%d" % t)
-            nc.scalar.activation(
-                out=ratio[t][:], in_=z_wave[t][:], func=FUNC.Tanh, bias=column(bias, Z, t)
-            )
-            output_wave[t] = whole_wave(OUTPUT, t)
-
-        gate_o = {}
+            fourth[t] = full.tile([P, BATCH], F32, tag="fourth", name="fourth_%d" % t)
+            nc.scalar.activation(out=fourth[t][:], in_=wave[t][:], func=FUNC.Tanh, bias=column(bias, Z, t))
+            wave[t] = whole_wave(OUTPUT, t)
 
         def output_gate(t):
-            gate_o[t] = work.tile([P, BATCH], F32, tag="gate_o", bufs=6, name="gate_o_%d" % t)
+            gate_o[t] = work.tile([P, BATCH], F32, tag="gate_o", bufs=8, name="gate_o_%d" % t)
             nc.scalar.activation(
-                out=gate_o[t][:], in_=output_wave[t][:], func=FUNC.Tanh,
+                out=gate_o[t][:], in_=wave[t][:], func=FUNC.Tanh,
                 bias=column(half_bias, OUTPUT, t), scale=0.5,
             )
 
         def finish_output_gate(t):
             nc.scalar.activation(out=gate_o[t][:], in_=gate_o[t][:], func=FUNC.Identity, bias=0.5, scale=0.5)
 
-        def divide_c(t):
-            nc.vector.tensor_tensor(
-                out=c_over_n1[t][:], in0=c_over_n1[t][:], in1=c_sb[:, t, :], op=ALU.mult
-            )
-
         def normaliser(t):
             nc.vector.scalar_tensor_tensor(
-                out=n_t[t][:], in0=n_sb[:, t, :], scalar=1.0, in1=n_t[t][:], op0=ALU.add, op1=ALU.min
+                out=second[t][:], in0=n_sb[:, t, :], scalar=1.0, in1=second[t][:], op0=ALU.add, op1=ALU.min
             )
-            store(n_out, t, n_t[t])
+            store(n_out, t, second[t])
 
         def weigh_z(t):
-            nc.vector.tensor_tensor(out=ratio[t][:], in0=ratio[t][:], in1=exp_g[t][:], op=ALU.mult)
+            nc.vector.scalar_tensor_tensor(
+                out=fourth[t][:], in0=first[t][:], scalar=math.exp(EXP_CLAMP), in1=fourth[t][:],
+                op0=ALU.min, op1=ALU.mult,
+            )
 
         def add_c(t):
-            nc.vector.tensor_tensor(out=ratio[t][:], in0=ratio[t][:], in1=c_over_n1[t][:], op=ALU.add)
+            wave[t] = psum.tile([P, BATCH], F32, tag="bank_%d" % t, name="sum_%d" % t)
+            nc.tensor.matmul(out=wave[t][:], lhsT=identity[:], rhs=c_sb[:, t, :], start=True, stop=False)
+            nc.tensor.matmul(out=wave[t][:], lhsT=identity_f32[:], rhs=fourth[t][:], start=False, stop=True)
 
-        def tanh_ratio(t):
-            nc.scalar.activation(out=ratio[t][:], in_=ratio[t][:], func=FUNC.Tanh)
+        def divide(t):
+            nc.vector.tensor_tensor(out=first[t][:], in0=wave[t][:], in1=third[t][:], op=ALU.mult)
 
         def cell(t):
-            c_t = full.tile([P, BATCH], F32, tag="lfm", name="c_t_%d" % t)
-            nc.vector.tensor_tensor(out=c_t[:], in0=n_t[t][:], in1=ratio[t][:], op=ALU.mult)
-            store(c_out, t, c_t)
+            nc.vector.tensor_tensor(out=fourth[t][:], in0=second[t][:], in1=first[t][:], op=ALU.mult)
+            store(c_out, t, fourth[t])
+
+        def tanh_ratio(t):
+            nc.scalar.activation(out=first[t][:], in_=first[t][:], func=FUNC.Tanh)
 
         def hidden(t):
-            nc.vector.tensor_tensor(out=ratio[t][:], in0=ratio[t][:], in1=gate_o[t][:], op=ALU.mult)
-            store(h_out, t, ratio[t])
+            nc.vector.tensor_tensor(out=first[t][:], in0=first[t][:], in1=gate_o[t][:], op=ALU.mult)
+            store(h_out, t, first[t])
 
-        def stage_1(pair):
-            alternate(pair, add_log_sigmoid, new_stabiliser, difference, exponent, z_matmuls)
-
-        def stage_2(pair):
-            alternate(pair, exp_plus, inverse_n1, exp_minus, tanh_z)
-
-        def stage_3(pair):
-            alternate(pair, output_gate, finish_output_gate, divide_c, normaliser, weigh_z, add_c, cell)
-
-        def stage_4(pair):
-            alternate(pair, tanh_ratio)
-
-        def stage_5(pair):
-            alternate(pair, hidden)
-
-        stages = (stage_1, stage_2, stage_3, stage_4, stage_5)
+        stages = (
+            (add_log_sigmoid, new_stabiliser, difference, exponent, z_matmuls),
+            (exp_plus, exp_minus, inverse_n1, tanh_z),
+            (output_gate, finish_output_gate, normaliser, weigh_z, add_c),
+            (divide, cell),
+            (tanh_ratio,),
+            (hidden,),
+        )
         for step in range(len(pairs) + len(stages) - 1):
-            for depth, stage_of_pair in enumerate(stages):
+            for depth, stage_steps in enumerate(stages):
                 if 0 <= step - depth < len(pairs):
-                    stage_of_pair(pairs[step - depth])
+                    alternate(pairs[step - depth], *stage_steps)

@@ -258,10 +258,9 @@ def tile_slstmcell_pa_kernel(
                 op0=ALU.add, op1=ALU.subtract,
             )
 
-        def exponent(t):
-            nc.vector.scalar_tensor_tensor(
-                out=second[t][:], in0=first[t][:], scalar=EXP_CLAMP, in1=third[t][:],
-                op0=ALU.min, op1=ALU.subtract,
+        def positive_part(t):
+            nc.vector.tensor_scalar(
+                out=second[t][:], in0=first[t][:], scalar1=0.0, scalar2=EXP_CLAMP, op0=ALU.max, op1=ALU.min
             )
 
         def z_matmuls(t):
@@ -270,7 +269,7 @@ def tile_slstmcell_pa_kernel(
         def exp_plus(t):
             nc.scalar.activation(out=first[t][:], in_=first[t][:], func=FUNC.Exp)
 
-        def exp_minus(t):
+        def forget_factor(t):
             nc.scalar.activation(out=second[t][:], in_=second[t][:], func=FUNC.Exp, scale=-1.0)
 
         def inverse_n1(t):
@@ -279,23 +278,15 @@ def tile_slstmcell_pa_kernel(
         def tanh_z(t):
             fourth[t] = full.tile([P, BATCH], F32, tag="fourth", name="fourth_%d" % t)
             nc.scalar.activation(out=fourth[t][:], in_=wave[t][:], func=FUNC.Tanh, bias=column(bias, Z, t))
+
+        def o_matmuls(t):
             wave[t] = whole_wave(OUTPUT, t)
 
         def output_gate(t):
-            gate_o[t] = work.tile([P, BATCH], F32, tag="gate_o", bufs=8, name="gate_o_%d" % t)
+            gate_o[t] = work.tile([P, BATCH], F32, tag="gate_o", bufs=4, name="gate_o_%d" % t)
             nc.scalar.activation(
-                out=gate_o[t][:], in_=wave[t][:], func=FUNC.Tanh,
-                bias=column(half_bias, OUTPUT, t), scale=0.5,
+                out=gate_o[t][:], in_=wave[t][:], func=FUNC.Sigmoid, bias=column(bias, OUTPUT, t)
             )
-
-        def finish_output_gate(t):
-            nc.scalar.activation(out=gate_o[t][:], in_=gate_o[t][:], func=FUNC.Identity, bias=0.5, scale=0.5)
-
-        def normaliser(t):
-            nc.vector.scalar_tensor_tensor(
-                out=second[t][:], in0=n_sb[:, t, :], scalar=1.0, in1=second[t][:], op0=ALU.add, op1=ALU.min
-            )
-            store(n_out, t, second[t])
 
         def weigh_z(t):
             nc.vector.scalar_tensor_tensor(
@@ -312,8 +303,14 @@ def tile_slstmcell_pa_kernel(
             nc.vector.tensor_tensor(out=first[t][:], in0=wave[t][:], in1=third[t][:], op=ALU.mult)
 
         def cell(t):
-            nc.vector.tensor_tensor(out=fourth[t][:], in0=second[t][:], in1=first[t][:], op=ALU.mult)
+            nc.vector.tensor_tensor(out=fourth[t][:], in0=wave[t][:], in1=second[t][:], op=ALU.mult)
             store(c_out, t, fourth[t])
+
+        def normaliser(t):
+            nc.vector.scalar_tensor_tensor(
+                out=second[t][:], in0=n_sb[:, t, :], scalar=1.0, in1=second[t][:], op0=ALU.add, op1=ALU.mult
+            )
+            store(n_out, t, second[t])
 
         def tanh_ratio(t):
             nc.scalar.activation(out=first[t][:], in_=first[t][:], func=FUNC.Tanh)
@@ -323,11 +320,12 @@ def tile_slstmcell_pa_kernel(
             store(h_out, t, first[t])
 
         stages = (
-            (add_log_sigmoid, new_stabiliser, difference, exponent, z_matmuls),
-            (exp_plus, exp_minus, inverse_n1, tanh_z),
-            (output_gate, finish_output_gate, normaliser, weigh_z, add_c),
-            (divide, cell),
+            (add_log_sigmoid, new_stabiliser, difference, positive_part, z_matmuls),
+            (exp_plus, forget_factor, inverse_n1, tanh_z),
+            (weigh_z, add_c),
+            (divide, cell, normaliser, o_matmuls),
             (tanh_ratio,),
+            (output_gate,),
             (hidden,),
         )
         for step in range(len(pairs) + len(stages) - 1):

@@ -148,11 +148,11 @@ def tile_slstmcell_pa_kernel(
                 stop=(k == PASSES - 1),
             )
 
-        def new_wave(gate, tile_index):
-            return psum.tile([P, BATCH], F32, tag="bank_%d" % tile_index, name="wave_%d_%d" % (gate, tile_index))
+        def new_wave(gate, tile_index, bank):
+            return psum.tile([P, BATCH], F32, tag="bank_%d" % bank, name="wave_%d_%d" % (gate, tile_index))
 
-        def whole_wave(gate, tile_index):
-            wave = new_wave(gate, tile_index)
+        def whole_wave(gate, tile_index, bank):
+            wave = new_wave(gate, tile_index, bank)
             for k in range(PASSES):
                 mx_pass(wave, gate, tile_index, k)
             return wave
@@ -201,7 +201,7 @@ def tile_slstmcell_pa_kernel(
         nc.vector.tensor_scalar_mul(out=minus_bias[:], in0=bias[:], scalar1=-1.0)
         quantise(regroup(nc.vector.tensor_copy, h_raws), HALVES)
 
-        forget_wave = [new_wave(FORGET, t) for t in range(TILES)]
+        forget_wave = [new_wave(FORGET, t, t) for t in range(TILES)]
         for k in range(HALVES):
             for t in range(TILES):
                 mx_pass(forget_wave[t], FORGET, t, k)
@@ -215,6 +215,7 @@ def tile_slstmcell_pa_kernel(
         fourth = {}
         gate_o = {}
         wave = {}
+        wave_o = {}
         for t in range(TILES):
             first[t] = full.tile([P, BATCH], F32, tag="first", name="first_%d" % t)
             nc.scalar.activation(
@@ -230,7 +231,7 @@ def tile_slstmcell_pa_kernel(
                 out=second[t][:], in0=forget_wave[t][:], scalar=column(minus_bias, FORGET, t),
                 in1=m_sb[:, t, :], op0=ALU.min, op1=ALU.add,
             )
-            wave[t] = whole_wave(INPUT, t)
+            wave[t] = whole_wave(INPUT, t, t)
 
         for t in range(TILES):
             nc.scalar.activation(out=first[t][:], in_=first[t][:], func=FUNC.Ln, bias=0.5, scale=0.5)
@@ -264,7 +265,7 @@ def tile_slstmcell_pa_kernel(
             )
 
         def z_matmuls(t):
-            wave[t] = whole_wave(Z, t)
+            wave[t] = whole_wave(Z, t, t)
 
         def exp_plus(t):
             nc.scalar.activation(out=first[t][:], in_=first[t][:], func=FUNC.Exp)
@@ -280,12 +281,12 @@ def tile_slstmcell_pa_kernel(
             nc.scalar.activation(out=fourth[t][:], in_=wave[t][:], func=FUNC.Tanh, bias=column(bias, Z, t))
 
         def o_matmuls(t):
-            wave[t] = whole_wave(OUTPUT, t)
+            wave_o[t] = whole_wave(OUTPUT, t, t % (TILES // 2))
 
         def output_gate(t):
             gate_o[t] = work.tile([P, BATCH], F32, tag="gate_o", bufs=4, name="gate_o_%d" % t)
             nc.scalar.activation(
-                out=gate_o[t][:], in_=wave[t][:], func=FUNC.Sigmoid, bias=column(bias, OUTPUT, t)
+                out=gate_o[t][:], in_=wave_o[t][:], func=FUNC.Sigmoid, bias=column(bias, OUTPUT, t)
             )
 
         def weigh_z(t):
@@ -324,8 +325,7 @@ def tile_slstmcell_pa_kernel(
             (exp_plus, forget_factor, inverse_n1, tanh_z),
             (weigh_z, add_c),
             (divide, cell, normaliser, o_matmuls),
-            (tanh_ratio,),
-            (output_gate,),
+            (tanh_ratio, output_gate),
             (hidden,),
         )
         for step in range(len(pairs) + len(stages) - 1):

@@ -23,6 +23,8 @@ HALVES = FEATURES // K_PASS
 PASSES = 2 * HALVES
 PLANE_ROWS = 4
 QUADRANTS = 4
+CHUNK = TILES // 2
+VECTOR_COLS = 336
 
 FORGET = 0
 INPUT = 1
@@ -74,7 +76,7 @@ def tile_slstmcell_pa_kernel(
                 words[(gate, operand)] = keep.tile(
                     [P, HALVES, FEATURES], U32, name="words_%d_%d" % (gate, operand), align_bytes=64
                 )
-        planes = keep.tile([P, GATES, 2, FEATURES], U8, align_bytes=64)
+        planes = keep.tile([P, GATES, FEATURES], U8, align_bytes=64)
         codes = keep.tile([P, PASSES, BATCH], U32, align_bytes=64)
         code_planes = keep.tile([P, PASSES, BATCH], U8, align_bytes=64)
         m_sb = keep.tile([P, TILES, BATCH], BF16)
@@ -90,20 +92,24 @@ def tile_slstmcell_pa_kernel(
         def by_tile(dram):
             return dram.rearrange("(t p) b -> p t b", p=P)
 
-        def load_weight(gate, operand):
+        def load_words(gate, operand, first_tile=0, tiles=TILES):
+            cols = slice(first_tile * P, (first_tile + tiles) * P)
             for half in range(HALVES):
                 nc.sync.dma_start(
-                    out=words[(gate, operand)][:, half, :].bitcast(I32),
-                    in_=dram_words[gate][operand][half].rearrange("p n t -> p (n t)").bitcast(I32),
+                    out=words[(gate, operand)][:, half, cols].bitcast(I32),
+                    in_=dram_words[gate][operand][half][:, cols, :].rearrange("p n t -> p (n t)").bitcast(I32),
                 )
-            scales = dram_scales[gate][operand]
-            queue, word = (nc.sync, I32) if gate == FORGET else (nc.gpsimd, F32)
-            for quadrant in range(QUADRANTS):
-                first = 32 * quadrant
-                queue.dma_start(
-                    out=planes[first : first + PLANE_ROWS * HALVES, gate, operand, :].bitcast(word),
-                    in_=scales[:, PLANE_ROWS * quadrant : PLANE_ROWS * (quadrant + 1), :].bitcast(word),
-                )
+
+        def load_scales(gate):
+            for operand in range(2):
+                for quadrant in range(QUADRANTS):
+                    first = 32 * quadrant + PLANE_ROWS * HALVES * operand
+                    nc.sync.dma_start(
+                        out=planes[first : first + PLANE_ROWS * HALVES, gate, :].bitcast(I32),
+                        in_=dram_scales[gate][operand][
+                            :, PLANE_ROWS * quadrant : PLANE_ROWS * (quadrant + 1), :
+                        ].bitcast(I32),
+                    )
 
         def load_rows(source):
             raws = []
@@ -114,16 +120,20 @@ def tile_slstmcell_pa_kernel(
                 raws.append(raw)
             return raws
 
-        def regroup(copy, raws):
+        def regroup(raws):
             groupeds = []
             for raw in raws:
                 grouped = stage.tile(
                     [P, BATCH, PACK], BF16, tag="grouped", bufs=PASSES, name="grouped", align_bytes=64
                 )
-                copy(
-                    out=grouped[:].rearrange("p (c i) j -> p c j i", i=4),
-                    in_=raw[:].rearrange("p j (c i) -> p c j i", i=4),
-                )
+                for copy, cols in (
+                    (nc.vector.tensor_copy, slice(0, VECTOR_COLS)),
+                    (nc.scalar.copy, slice(VECTOR_COLS, BATCH)),
+                ):
+                    copy(
+                        out=grouped[:, cols, :].rearrange("p (c i) j -> p c j i", i=4),
+                        in_=raw[:, :, cols].rearrange("p j (c i) -> p c j i", i=4),
+                    )
                 groupeds.append(grouped)
             return groupeds
 
@@ -141,7 +151,7 @@ def tile_slstmcell_pa_kernel(
             nc.tensor.matmul_mx(
                 out=wave[:],
                 lhsT=words[(gate, operand)][:, half, cols].bitcast(FP8X4),
-                lhsT_scale=planes[PLANE_ROWS * half : P, gate, operand, cols],
+                lhsT_scale=planes[PLANE_ROWS * k : P, gate, cols],
                 rhs=codes[:, k, :].bitcast(FP8X4),
                 rhs_scale=code_planes[:, k, :],
                 start=(k == 0),
@@ -180,33 +190,43 @@ def tile_slstmcell_pa_kernel(
                 in_=dram_bias[gate].rearrange("(t p) -> t p", p=P),
             )
         x_raws = load_rows(x)
-        load_weight(FORGET, 0)
+        load_scales(FORGET)
+        load_words(FORGET, 0, 0, CHUNK)
         h_raws = load_rows(h_prev)
-        load_weight(FORGET, 1)
-        nc.sync.dma_start(out=m_sb[:], in_=by_tile(m_prev))
-        load_weight(INPUT, 0)
-        load_weight(INPUT, 1)
+        load_words(FORGET, 1, 0, CHUNK)
+        nc.sync.dma_start(out=m_sb[:, 0:CHUNK, :], in_=by_tile(m_prev)[:, 0:CHUNK, :])
+        load_words(FORGET, 0, CHUNK, CHUNK)
+        load_words(FORGET, 1, CHUNK, CHUNK)
+        nc.sync.dma_start(out=m_sb[:, CHUNK:TILES, :], in_=by_tile(m_prev)[:, CHUNK:TILES, :])
+        load_scales(INPUT)
+        load_words(INPUT, 0)
+        load_words(INPUT, 1)
         nc.sync.dma_start(out=n_sb[:], in_=by_tile(n_prev))
-        load_weight(Z, 0)
-        load_weight(Z, 1)
+        load_scales(Z)
+        load_words(Z, 0)
+        load_words(Z, 1)
         nc.sync.dma_start(out=c_sb[:], in_=by_tile(c_prev))
-        load_weight(OUTPUT, 0)
-        load_weight(OUTPUT, 1)
+        load_scales(OUTPUT)
+        load_words(OUTPUT, 0)
+        load_words(OUTPUT, 1)
 
         bias_columns = psum.tile([P, P], BF16, tag="bank_%d" % (TILES - 1))
         nc.tensor.transpose(bias_columns[:], bias_rows[:], identity[:])
-        quantise(regroup(nc.vector.tensor_copy, x_raws), 0)
+        quantise(regroup(x_raws), 0)
         nc.vector.tensor_copy(out=bias[:], in_=bias_columns[:, 0 : GATES * TILES])
         nc.vector.tensor_scalar_mul(out=half_bias[:], in0=bias[:], scalar1=0.5)
         nc.vector.tensor_scalar_mul(out=minus_bias[:], in0=bias[:], scalar1=-1.0)
-        quantise(regroup(nc.vector.tensor_copy, h_raws), HALVES)
+        quantise(regroup(h_raws), HALVES)
 
         forget_wave = [new_wave(FORGET, t, t) for t in range(TILES)]
         for k in range(HALVES):
-            for t in range(TILES):
+            for t in range(CHUNK):
                 mx_pass(forget_wave[t], FORGET, t, k)
-        for t in range(TILES):
+        for t in range(CHUNK):
             for k in range(HALVES, PASSES):
+                mx_pass(forget_wave[t], FORGET, t, k)
+        for t in range(CHUNK, TILES):
+            for k in range(PASSES):
                 mx_pass(forget_wave[t], FORGET, t, k)
 
         first = {}

@@ -76,7 +76,7 @@ def tile_slstmcell_pa_kernel(
                 words[(gate, operand)] = keep.tile(
                     [P, HALVES, FEATURES], U32, name="words_%d_%d" % (gate, operand), align_bytes=64
                 )
-        planes = keep.tile([P, GATES, FEATURES], U8, align_bytes=64)
+        planes = keep.tile([P, GATES, 2, FEATURES], U8, align_bytes=64)
         codes = keep.tile([P, PASSES, BATCH], U32, align_bytes=64)
         code_planes = keep.tile([P, PASSES, BATCH], U8, align_bytes=64)
         m_sb = keep.tile([P, TILES, BATCH], BF16)
@@ -92,24 +92,25 @@ def tile_slstmcell_pa_kernel(
         def by_tile(dram):
             return dram.rearrange("(t p) b -> p t b", p=P)
 
-        def load_words(gate, operand, first_tile=0, tiles=TILES):
+        def load_half(gate, operand, half, first_tile=0, tiles=TILES):
             cols = slice(first_tile * P, (first_tile + tiles) * P)
-            for half in range(HALVES):
-                nc.sync.dma_start(
-                    out=words[(gate, operand)][:, half, cols].bitcast(I32),
-                    in_=dram_words[gate][operand][half][:, cols, :].rearrange("p n t -> p (n t)").bitcast(I32),
-                )
+            nc.sync.dma_start(
+                out=words[(gate, operand)][:, half, cols].bitcast(I32),
+                in_=dram_words[gate][operand][half][:, cols, :].rearrange("p n t -> p (n t)").bitcast(I32),
+            )
 
-        def load_scales(gate):
-            for operand in range(2):
-                for quadrant in range(QUADRANTS):
-                    first = 32 * quadrant + PLANE_ROWS * HALVES * operand
-                    nc.sync.dma_start(
-                        out=planes[first : first + PLANE_ROWS * HALVES, gate, :].bitcast(I32),
-                        in_=dram_scales[gate][operand][
-                            :, PLANE_ROWS * quadrant : PLANE_ROWS * (quadrant + 1), :
-                        ].bitcast(I32),
-                    )
+        def load_scale_rows(gate, operand, quadrant):
+            first = 32 * quadrant
+            nc.sync.dma_start(
+                out=planes[first : first + PLANE_ROWS * HALVES, gate, operand, :].bitcast(I32),
+                in_=dram_scales[gate][operand][
+                    :, PLANE_ROWS * quadrant : PLANE_ROWS * (quadrant + 1), :
+                ].bitcast(I32),
+            )
+
+        def load_state(state_sb, state, first_tile=0, tiles=TILES):
+            chosen = slice(first_tile, first_tile + tiles)
+            nc.sync.dma_start(out=state_sb[:, chosen, :], in_=by_tile(state)[:, chosen, :])
 
         def load_rows(source):
             raws = []
@@ -151,7 +152,7 @@ def tile_slstmcell_pa_kernel(
             nc.tensor.matmul_mx(
                 out=wave[:],
                 lhsT=words[(gate, operand)][:, half, cols].bitcast(FP8X4),
-                lhsT_scale=planes[PLANE_ROWS * k : P, gate, cols],
+                lhsT_scale=planes[PLANE_ROWS * half : P, gate, operand, cols],
                 rhs=codes[:, k, :].bitcast(FP8X4),
                 rhs_scale=code_planes[:, k, :],
                 start=(k == 0),
@@ -180,8 +181,9 @@ def tile_slstmcell_pa_kernel(
 
         pairs = [(t, t + 1) for t in range(0, TILES, 2)]
 
-        nc.vector.memset(planes[:].bitcast(I32), 0)
         nc.vector.memset(bias_rows[:], 0.0)
+        nc.vector.memset(planes[:, FORGET, :, :].bitcast(I32), 0)
+        nc.vector.memset(planes[:, FORGET + 1 : GATES, :, :].bitcast(I32), 0)
         make_identity(nc, identity[:])
         make_identity(nc, identity_f32[:])
         for gate in range(GATES):
@@ -190,25 +192,35 @@ def tile_slstmcell_pa_kernel(
                 in_=dram_bias[gate].rearrange("(t p) -> t p", p=P),
             )
         x_raws = load_rows(x)
-        load_scales(FORGET)
-        load_words(FORGET, 0, 0, CHUNK)
+        for half in range(HALVES):
+            load_half(FORGET, 0, half, 0, CHUNK)
+        for quadrant in range(QUADRANTS):
+            load_scale_rows(FORGET, 0, quadrant)
         h_raws = load_rows(h_prev)
-        load_words(FORGET, 1, 0, CHUNK)
-        nc.sync.dma_start(out=m_sb[:, 0:CHUNK, :], in_=by_tile(m_prev)[:, 0:CHUNK, :])
-        load_words(FORGET, 0, CHUNK, CHUNK)
-        load_words(FORGET, 1, CHUNK, CHUNK)
-        nc.sync.dma_start(out=m_sb[:, CHUNK:TILES, :], in_=by_tile(m_prev)[:, CHUNK:TILES, :])
-        load_scales(INPUT)
-        load_words(INPUT, 0)
-        load_words(INPUT, 1)
-        nc.sync.dma_start(out=n_sb[:], in_=by_tile(n_prev))
-        load_scales(Z)
-        load_words(Z, 0)
-        load_words(Z, 1)
-        nc.sync.dma_start(out=c_sb[:], in_=by_tile(c_prev))
-        load_scales(OUTPUT)
-        load_words(OUTPUT, 0)
-        load_words(OUTPUT, 1)
+        for half in range(HALVES):
+            load_half(FORGET, 1, half, 0, CHUNK)
+        for quadrant in range(QUADRANTS):
+            load_scale_rows(FORGET, 1, quadrant)
+        large = [(load_state, (m_sb, m_prev, 0, CHUNK))]
+        large.extend((load_half, (FORGET, operand, half, CHUNK, CHUNK)) for operand in range(2) for half in range(HALVES))
+        large.append((load_state, (m_sb, m_prev, CHUNK, CHUNK)))
+        for gate, state_sb, state in ((INPUT, n_sb, n_prev), (Z, c_sb, c_prev), (OUTPUT, None, None)):
+            large.extend((load_half, (gate, operand, half)) for operand in range(2) for half in range(HALVES))
+            if state is not None:
+                large.append((load_state, (state_sb, state)))
+        small = [
+            (gate, operand, quadrant)
+            for gate in (INPUT, Z, OUTPUT)
+            for operand in range(2)
+            for quadrant in range(QUADRANTS)
+        ]
+        taken = 0
+        for number, (load, arguments) in enumerate(large):
+            load(*arguments)
+            for repeat in range(2 if 8 <= number < 12 else 1):
+                if taken < len(small):
+                    load_scale_rows(*small[taken])
+                    taken += 1
 
         bias_columns = psum.tile([P, P], BF16, tag="bank_%d" % (TILES - 1))
         nc.tensor.transpose(bias_columns[:], bias_rows[:], identity[:])
@@ -242,16 +254,15 @@ def tile_slstmcell_pa_kernel(
                 out=first[t][:], in_=forget_wave[t][:], func=FUNC.Tanh,
                 bias=column(half_bias, FORGET, t), scale=0.5,
             )
-            nc.vector.scalar_tensor_tensor(
-                out=first[t][:], in0=first[t][:], scalar=-1.0, in1=first[t][:], op0=ALU.mult, op1=ALU.max
-            )
-        for t in range(TILES):
             second[t] = full.tile([P, BATCH], F32, tag="second", name="second_%d" % t)
             nc.vector.scalar_tensor_tensor(
                 out=second[t][:], in0=forget_wave[t][:], scalar=column(minus_bias, FORGET, t),
                 in1=m_sb[:, t, :], op0=ALU.min, op1=ALU.add,
             )
             wave[t] = whole_wave(INPUT, t, t)
+            nc.vector.scalar_tensor_tensor(
+                out=first[t][:], in0=first[t][:], scalar=-1.0, in1=first[t][:], op0=ALU.mult, op1=ALU.max
+            )
 
         for t in range(TILES):
             nc.scalar.activation(out=first[t][:], in_=first[t][:], func=FUNC.Ln, bias=0.5, scale=0.5)
@@ -266,7 +277,7 @@ def tile_slstmcell_pa_kernel(
             )
 
         def new_stabiliser(t):
-            m_t = work.tile([P, BATCH], F32, tag="m_t", bufs=5)
+            m_t = work.tile([P, BATCH], F32, tag="m_t", bufs=TILES)
             nc.vector.scalar_tensor_tensor(
                 out=m_t[:], in0=wave[t][:], scalar=column(bias, INPUT, t), in1=second[t][:],
                 op0=ALU.add, op1=ALU.max,

@@ -353,7 +353,7 @@ def tile_slstmcell_pa_kernel(
 
         stages = (
             (add_log_sigmoid, new_stabiliser, difference, positive_part, z_matmuls),
-            (exp_plus, forget_factor, inverse_n1, tanh_z),
+            (exp_plus, tanh_z, forget_factor, inverse_n1),
             (weigh_z, add_c),
             (divide, cell, normaliser, o_matmuls),
             (tanh_ratio, output_gate),

@@ -112,12 +112,12 @@ def tile_slstmcell_pa_kernel(
             chosen = slice(first_tile, first_tile + tiles)
             nc.sync.dma_start(out=state_sb[:, chosen, :], in_=by_tile(state)[:, chosen, :])
 
-        def load_rows(source):
+        def load_rows(queue, source):
             raws = []
             for half in range(HALVES):
                 raw = stage.tile([P, PACK, BATCH], BF16, tag="raw", bufs=PASSES, name="raw")
                 rows = source[half * K_PASS : (half + 1) * K_PASS, :]
-                nc.sync.dma_start(out=raw[:], in_=rows.rearrange("(p j) b -> p j b", j=PACK))
+                queue.dma_start(out=raw[:], in_=rows.rearrange("(p j) b -> p j b", j=PACK))
                 raws.append(raw)
             return raws
 
@@ -184,6 +184,7 @@ def tile_slstmcell_pa_kernel(
         nc.vector.memset(bias_rows[:], 0.0)
         nc.vector.memset(planes[:, FORGET, :, :].bitcast(I32), 0)
         nc.vector.memset(planes[:, FORGET + 1 : GATES, :, :].bitcast(I32), 0)
+        h_raws = load_rows(nc.gpsimd, h_prev)
         make_identity(nc, identity[:])
         make_identity(nc, identity_f32[:])
         for gate in range(GATES):
@@ -191,12 +192,11 @@ def tile_slstmcell_pa_kernel(
                 out=bias_rows[TILES * gate : TILES * (gate + 1), :],
                 in_=dram_bias[gate].rearrange("(t p) -> t p", p=P),
             )
-        x_raws = load_rows(x)
+        x_raws = load_rows(nc.sync, x)
         for half in range(HALVES):
             load_half(FORGET, 0, half, 0, CHUNK)
         for quadrant in range(QUADRANTS):
             load_scale_rows(FORGET, 0, quadrant)
-        h_raws = load_rows(h_prev)
         for half in range(HALVES):
             load_half(FORGET, 1, half, 0, CHUNK)
         for quadrant in range(QUADRANTS):

@@ -34,6 +34,10 @@ GATES = 4
 
 EXP_CLAMP = 80.0
 
+SPLIT = 20.0
+
+WARM_UP_MATMULS = 10
+
 FLOPS = 2 * 2 * GATES * FEATURES * FEATURES * BATCH
 
 
@@ -82,21 +86,31 @@ def tile_slstmcell_pa_kernel(
         m_sb = keep.tile([P, TILES, BATCH], BF16)
         n_sb = keep.tile([P, TILES, BATCH], BF16)
         c_sb = keep.tile([P, TILES, BATCH], BF16)
+        forget_bias_row = keep.tile([P, P], BF16)
         bias_rows = keep.tile([P, P], BF16)
         identity = keep.tile([P, P], BF16)
         identity_f32 = keep.tile([P, P], F32)
         bias = keep.tile([P, GATES * TILES], F32)
-        half_bias = keep.tile([P, GATES * TILES], F32)
-        minus_bias = keep.tile([P, GATES * TILES], F32)
+        forget_bias = keep.tile([P, TILES], F32)
+        bias_split = keep.tile([P, TILES], F32)
+        minus_bias_split = keep.tile([P, TILES], F32)
+        warm = keep.tile([P, 1], F32)
+        idle_rows = keep.tile([P, BATCH], BF16)
 
         def by_tile(dram):
             return dram.rearrange("(t p) b -> p t b", p=P)
 
-        def load_half(gate, operand, half, first_tile=0, tiles=TILES):
-            cols = slice(first_tile * P, (first_tile + tiles) * P)
+        def load_half(gate, operand, half):
             nc.sync.dma_start(
-                out=words[(gate, operand)][:, half, cols].bitcast(I32),
-                in_=dram_words[gate][operand][half][:, cols, :].rearrange("p n t -> p (n t)").bitcast(I32),
+                out=words[(gate, operand)][:, half, :].bitcast(I32),
+                in_=dram_words[gate][operand][half].rearrange("p n t -> p (n t)").bitcast(I32),
+            )
+
+        def load_range(gate, operand, first_tile):
+            cols = slice(first_tile * P, (first_tile + CHUNK) * P)
+            nc.sync.dma_start(
+                out=words[(gate, operand)][:, :, cols].bitcast(I32),
+                in_=dram_words[gate][operand][:, :, cols, :].rearrange("g p n t -> p g (n t)").bitcast(I32),
             )
 
         def load_scale_rows(gate, operand, quadrant):
@@ -112,39 +126,32 @@ def tile_slstmcell_pa_kernel(
             chosen = slice(first_tile, first_tile + tiles)
             nc.sync.dma_start(out=state_sb[:, chosen, :], in_=by_tile(state)[:, chosen, :])
 
-        def load_rows(queue, source):
-            raws = []
-            for half in range(HALVES):
-                raw = stage.tile([P, PACK, BATCH], BF16, tag="raw", bufs=PASSES, name="raw")
-                rows = source[half * K_PASS : (half + 1) * K_PASS, :]
-                queue.dma_start(out=raw[:], in_=rows.rearrange("(p j) b -> p j b", j=PACK))
-                raws.append(raw)
-            return raws
+        def load_rows(source, half):
+            raw = stage.tile([P, PACK, BATCH], BF16, tag="raw", bufs=PASSES, name="raw")
+            rows = source[half * K_PASS : (half + 1) * K_PASS, :]
+            nc.sync.dma_start(out=raw[:], in_=rows.rearrange("(p j) b -> p j b", j=PACK))
+            return raw
 
-        def regroup(raws):
-            groupeds = []
-            for raw in raws:
-                grouped = stage.tile(
-                    [P, BATCH, PACK], BF16, tag="grouped", bufs=PASSES, name="grouped", align_bytes=64
+        def regroup(raw):
+            grouped = stage.tile(
+                [P, BATCH, PACK], BF16, tag="grouped", bufs=PASSES, name="grouped", align_bytes=64
+            )
+            for copy, cols in (
+                (nc.vector.tensor_copy, slice(0, VECTOR_COLS)),
+                (nc.scalar.copy, slice(VECTOR_COLS, BATCH)),
+            ):
+                copy(
+                    out=grouped[:, cols, :].rearrange("p (c i) j -> p c j i", i=4),
+                    in_=raw[:, :, cols].rearrange("p j (c i) -> p c j i", i=4),
                 )
-                for copy, cols in (
-                    (nc.vector.tensor_copy, slice(0, VECTOR_COLS)),
-                    (nc.scalar.copy, slice(VECTOR_COLS, BATCH)),
-                ):
-                    copy(
-                        out=grouped[:, cols, :].rearrange("p (c i) j -> p c j i", i=4),
-                        in_=raw[:, :, cols].rearrange("p j (c i) -> p c j i", i=4),
-                    )
-                groupeds.append(grouped)
-            return groupeds
+            return grouped
 
-        def quantise(groupeds, first_pass):
-            for half in range(HALVES):
-                nc.vector.quantize_mx(
-                    out=codes[:, first_pass + half, :].bitcast(FP8X4),
-                    scales=code_planes[:, first_pass + half, :],
-                    in_=groupeds[half][:].rearrange("p b j -> p (b j)"),
-                )
+        def quantise(grouped, k):
+            nc.vector.quantize_mx(
+                out=codes[:, k, :].bitcast(FP8X4),
+                scales=code_planes[:, k, :],
+                in_=grouped[:].rearrange("p b j -> p (b j)"),
+            )
 
         def mx_pass(wave, gate, tile_index, k):
             operand, half = divmod(k, HALVES)
@@ -181,64 +188,95 @@ def tile_slstmcell_pa_kernel(
 
         pairs = [(t, t + 1) for t in range(0, TILES, 2)]
 
+        nc.vector.memset(forget_bias_row[:], 0.0)
         nc.vector.memset(bias_rows[:], 0.0)
+        nc.vector.memset(warm[:], 0.0)
+        nc.vector.memset(idle_rows[:], 0.0)
         nc.vector.memset(planes[:, FORGET, :, :].bitcast(I32), 0)
         nc.vector.memset(planes[:, FORGET + 1 : GATES, :, :].bitcast(I32), 0)
-        h_raws = load_rows(nc.gpsimd, h_prev)
-        make_identity(nc, identity[:])
-        make_identity(nc, identity_f32[:])
-        for gate in range(GATES):
-            nc.scalar.dma_start(
-                out=bias_rows[TILES * gate : TILES * (gate + 1), :],
+        nc.scalar.activation(out=warm[:], in_=warm[:], func=FUNC.Sigmoid)
+        def load_bias(rows, gate):
+            nc.gpsimd.dma_start(
+                out=rows[TILES * gate : TILES * (gate + 1), :],
                 in_=dram_bias[gate].rearrange("(t p) -> t p", p=P),
             )
-        x_raws = load_rows(nc.sync, x)
-        for half in range(HALVES):
-            load_half(FORGET, 0, half, 0, CHUNK)
+
+        load_bias(forget_bias_row, FORGET)
+        make_identity(nc, identity[:])
+        for gate in (INPUT, Z, OUTPUT):
+            load_bias(bias_rows, gate)
+        make_identity(nc, identity_f32[:])
+        x_raws = [load_rows(x, half) for half in range(HALVES)]
         for quadrant in range(QUADRANTS):
             load_scale_rows(FORGET, 0, quadrant)
-        for half in range(HALVES):
-            load_half(FORGET, 1, half, 0, CHUNK)
+        load_range(FORGET, 0, 0)
+        h_raws = [load_rows(h_prev, 0)]
+        h_raws.append(load_rows(h_prev, 1))
+        load_range(FORGET, 0, CHUNK)
         for quadrant in range(QUADRANTS):
             load_scale_rows(FORGET, 1, quadrant)
-        large = [(load_state, (m_sb, m_prev, 0, CHUNK))]
-        large.extend((load_half, (FORGET, operand, half, CHUNK, CHUNK)) for operand in range(2) for half in range(HALVES))
-        large.append((load_state, (m_sb, m_prev, CHUNK, CHUNK)))
-        for gate, state_sb, state in ((INPUT, n_sb, n_prev), (Z, c_sb, c_prev), (OUTPUT, None, None)):
-            large.extend((load_half, (gate, operand, half)) for operand in range(2) for half in range(HALVES))
-            if state is not None:
-                large.append((load_state, (state_sb, state)))
-        small = [
-            (gate, operand, quadrant)
-            for gate in (INPUT, Z, OUTPUT)
-            for operand in range(2)
-            for quadrant in range(QUADRANTS)
-        ]
-        taken = 0
-        for number, (load, arguments) in enumerate(large):
-            load(*arguments)
-            for repeat in range(2 if 8 <= number < 12 else 1):
-                if taken < len(small):
-                    load_scale_rows(*small[taken])
-                    taken += 1
+        load_range(FORGET, 1, 0)
+        load_state(m_sb, m_prev, 0, CHUNK)
+        load_range(FORGET, 1, CHUNK)
+        load_state(m_sb, m_prev, CHUNK, CHUNK)
+        load_range(INPUT, 0, 0)
+        for quadrant in range(QUADRANTS):
+            load_scale_rows(INPUT, 0, quadrant)
+        load_range(INPUT, 1, 0)
+        for quadrant in range(QUADRANTS):
+            load_scale_rows(INPUT, 1, quadrant)
+        load_range(INPUT, 0, CHUNK)
+        load_range(INPUT, 1, CHUNK)
+        load_state(n_sb, n_prev, 0, CHUNK)
+        load_state(n_sb, n_prev, CHUNK, CHUNK)
+        for operand in range(2):
+            for quadrant in range(QUADRANTS):
+                load_scale_rows(Z, operand, quadrant)
+            for half in range(HALVES):
+                load_half(Z, operand, half)
+        load_state(c_sb, c_prev, 0, CHUNK)
+        load_state(c_sb, c_prev, CHUNK, CHUNK)
+        for operand in range(2):
+            for quadrant in range(QUADRANTS):
+                load_scale_rows(OUTPUT, operand, quadrant)
+            for half in range(HALVES):
+                load_half(OUTPUT, operand, half)
 
-        bias_columns = psum.tile([P, P], BF16, tag="bank_%d" % (TILES - 1))
-        nc.tensor.transpose(bias_columns[:], bias_rows[:], identity[:])
-        quantise(regroup(x_raws), 0)
-        nc.vector.tensor_copy(out=bias[:], in_=bias_columns[:, 0 : GATES * TILES])
-        nc.vector.tensor_scalar_mul(out=half_bias[:], in0=bias[:], scalar1=0.5)
-        nc.vector.tensor_scalar_mul(out=minus_bias[:], in0=bias[:], scalar1=-1.0)
-        quantise(regroup(h_raws), HALVES)
+        warm_up = psum.tile([P, BATCH], F32, tag="bank_%d" % (TILES - 1), name="warm_up")
+        for repeat in range(WARM_UP_MATMULS):
+            nc.tensor.matmul(out=warm_up[:], lhsT=idle_rows[:, 0:P], rhs=idle_rows[:], start=True, stop=True)
 
-        forget_wave = [new_wave(FORGET, t, t) for t in range(TILES)]
+        forget_columns = psum.tile([P, P], BF16, tag="bank_%d" % (TILES - 2))
+        nc.tensor.transpose(forget_columns[:], forget_bias_row[:], identity[:])
+
+        x_grouped = [regroup(raw) for raw in x_raws]
+        for half in range(HALVES):
+            quantise(x_grouped[half], half)
+        h_grouped = [regroup(raw) for raw in h_raws]
+        for half in range(HALVES):
+            quantise(h_grouped[half], HALVES + half)
+        nc.vector.tensor_copy(out=forget_bias[:], in_=forget_columns[:, 0:TILES])
+        nc.vector.tensor_scalar_add(out=bias_split[:], in0=forget_bias[:], scalar1=SPLIT)
+        nc.vector.tensor_scalar_mul(out=minus_bias_split[:], in0=bias_split[:], scalar1=-1.0)
+
+        forget_wave = [new_wave(FORGET, t, t) for t in range(CHUNK)]
         for k in range(HALVES):
             for t in range(CHUNK):
+                mx_pass(forget_wave[t], FORGET, t, k)
+        w_ahead = CHUNK + 2
+        for t in range(CHUNK, w_ahead):
+            forget_wave.append(new_wave(FORGET, t, t))
+            for k in range(HALVES):
                 mx_pass(forget_wave[t], FORGET, t, k)
         for t in range(CHUNK):
             for k in range(HALVES, PASSES):
                 mx_pass(forget_wave[t], FORGET, t, k)
+        for t in range(w_ahead, TILES):
+            forget_wave.append(new_wave(FORGET, t, t))
+            for k in range(HALVES):
+                mx_pass(forget_wave[t], FORGET, t, k)
         for t in range(CHUNK, TILES):
-            for k in range(PASSES):
+            for k in range(HALVES, PASSES):
                 mx_pass(forget_wave[t], FORGET, t, k)
 
         first = {}
@@ -248,32 +286,47 @@ def tile_slstmcell_pa_kernel(
         gate_o = {}
         wave = {}
         wave_o = {}
+
+        def add_split(t):
+            nc.vector.tensor_scalar_add(out=second[t][:], in0=second[t][:], scalar1=bias_split[:, t : t + 1])
+
         for t in range(TILES):
             first[t] = full.tile([P, BATCH], F32, tag="first", name="first_%d" % t)
             nc.scalar.activation(
-                out=first[t][:], in_=forget_wave[t][:], func=FUNC.Tanh,
-                bias=column(half_bias, FORGET, t), scale=0.5,
+                out=first[t][:], in_=forget_wave[t][:], func=FUNC.Sigmoid, bias=forget_bias[:, t : t + 1]
             )
             second[t] = full.tile([P, BATCH], F32, tag="second", name="second_%d" % t)
             nc.vector.scalar_tensor_tensor(
-                out=second[t][:], in0=forget_wave[t][:], scalar=column(minus_bias, FORGET, t),
+                out=second[t][:], in0=forget_wave[t][:], scalar=minus_bias_split[:, t : t + 1],
                 in1=m_sb[:, t, :], op0=ALU.min, op1=ALU.add,
             )
-            wave[t] = whole_wave(INPUT, t, t)
-            nc.vector.scalar_tensor_tensor(
-                out=first[t][:], in0=first[t][:], scalar=-1.0, in1=first[t][:], op0=ALU.mult, op1=ALU.max
-            )
+            if t > 0:
+                add_split(t - 1)
+
+        add_split(TILES - 1)
+        bias_columns = psum.tile([P, P], BF16, tag="bank_%d" % (CHUNK - 1))
+        nc.tensor.transpose(bias_columns[:], bias_rows[:], identity[:])
+        nc.vector.tensor_copy(out=bias[:], in_=bias_columns[:, 0 : GATES * TILES])
+        for first_tile in range(0, TILES, CHUNK):
+            chunk = range(first_tile, first_tile + CHUNK)
+            for t in chunk:
+                wave[t] = new_wave(INPUT, t, t)
+                for k in range(HALVES):
+                    mx_pass(wave[t], INPUT, t, k)
+            for t in chunk:
+                for k in range(HALVES, PASSES):
+                    mx_pass(wave[t], INPUT, t, k)
 
         for t in range(TILES):
-            nc.scalar.activation(out=first[t][:], in_=first[t][:], func=FUNC.Ln, bias=0.5, scale=0.5)
+            nc.scalar.activation(out=first[t][:], in_=first[t][:], func=FUNC.Ln)
         for t in range(TILES):
             third[t] = full.tile([P, BATCH], F32, tag="third", name="third_%d" % t)
             nc.scalar.activation(out=third[t][:], in_=n_sb[:, t, :], func=FUNC.Ln, bias=1.0, scale=1.0)
 
         def add_log_sigmoid(t):
             nc.vector.scalar_tensor_tensor(
-                out=second[t][:], in0=second[t][:], scalar=column(bias, FORGET, t), in1=first[t][:],
-                op0=ALU.add, op1=ALU.add,
+                out=second[t][:], in0=first[t][:], scalar=-SPLIT, in1=second[t][:],
+                op0=ALU.max, op1=ALU.add,
             )
 
         def new_stabiliser(t):

import math
from contextlib import ExitStack

import concourse.mybir as mybir
from concourse.masks import make_identity

F32 = mybir.dt.float32
BF16 = mybir.dt.bfloat16
I32 = mybir.dt.int32
U32 = mybir.dt.uint32
U8 = mybir.dt.uint8
FP8X4 = mybir.dt.float8_e4m3fn_x4
FUNC = mybir.ActivationFunctionType
ALU = mybir.AluOpType

P = 128
FEATURES = 1024
BATCH = 512
TILES = FEATURES // P
PACK = 4
K_PASS = P * PACK
HALVES = FEATURES // K_PASS
PASSES = 2 * HALVES
PLANE_ROWS = 4
QUADRANTS = 4
CHUNK = TILES // 2
VECTOR_COLS = 336

FORGET = 0
INPUT = 1
Z = 2
OUTPUT = 3
GATES = 4

EXP_CLAMP = 80.0

SPLIT = 20.0

WARM_UP_MATMULS = 10

FLOPS = 2 * 2 * GATES * FEATURES * FEATURES * BATCH


def tile_slstmcell_pa_kernel(
    tc, x, h_prev, c_prev, n_prev, m_prev,
    w_input_words, w_input_scales, w_forget_words, w_forget_scales,
    w_output_words, w_output_scales, w_z_words, w_z_scales,
    r_input_words, r_input_scales, r_forget_words, r_forget_scales,
    r_output_words, r_output_scales, r_z_words, r_z_scales,
    b_input, b_forget, b_output, b_z,
    out_0, out_1, out_2, out_3,
):
    nc = tc.nc
    h_out, c_out, n_out, m_out = out_0, out_1, out_2, out_3
    dram_words = {
        FORGET: (w_forget_words, r_forget_words),
        INPUT: (w_input_words, r_input_words),
        Z: (w_z_words, r_z_words),
        OUTPUT: (w_output_words, r_output_words),
    }
    dram_scales = {
        FORGET: (w_forget_scales, r_forget_scales),
        INPUT: (w_input_scales, r_input_scales),
        Z: (w_z_scales, r_z_scales),
        OUTPUT: (w_output_scales, r_output_scales),
    }
    dram_bias = {FORGET: b_forget, INPUT: b_input, Z: b_z, OUTPUT: b_output}

    with ExitStack() as ctx:
        ctx.enter_context(tc.manual_schedule())
        keep = ctx.enter_context(tc.tile_pool(name="keep", bufs=1))
        stage = ctx.enter_context(tc.tile_pool(name="stage", bufs=2))
        full = ctx.enter_context(tc.tile_pool(name="full", bufs=TILES))
        work = ctx.enter_context(tc.tile_pool(name="work", bufs=3))
        psum = ctx.enter_context(tc.psum_pool(name="psum", bufs=1))

        words = {}
        for gate in range(GATES):
            for operand in range(2):
                words[(gate, operand)] = keep.tile(
                    [P, HALVES, FEATURES], U32, name="words_%d_%d" % (gate, operand), align_bytes=64
                )
        planes = keep.tile([P, GATES, 2, FEATURES], U8, align_bytes=64)
        codes = keep.tile([P, PASSES, BATCH], U32, align_bytes=64)
        code_planes = keep.tile([P, PASSES, BATCH], U8, align_bytes=64)
        m_sb = keep.tile([P, TILES, BATCH], BF16)
        n_sb = keep.tile([P, TILES, BATCH], BF16)
        c_sb = keep.tile([P, TILES, BATCH], BF16)
        forget_bias_row = keep.tile([P, P], BF16)
        bias_rows = keep.tile([P, P], BF16)
        identity = keep.tile([P, P], BF16)
        identity_f32 = keep.tile([P, P], F32)
        bias = keep.tile([P, GATES * TILES], F32)
        forget_bias = keep.tile([P, TILES], F32)
        bias_split = keep.tile([P, TILES], F32)
        minus_bias_split = keep.tile([P, TILES], F32)
        warm = keep.tile([P, 1], F32)
        idle_rows = keep.tile([P, BATCH], BF16)

        def by_tile(dram):
            return dram.rearrange("(t p) b -> p t b", p=P)

        def load_half(gate, operand, half):
            nc.sync.dma_start(
                out=words[(gate, operand)][:, half, :].bitcast(I32),
                in_=dram_words[gate][operand][half].rearrange("p n t -> p (n t)").bitcast(I32),
            )

        def load_range(gate, operand, first_tile):
            cols = slice(first_tile * P, (first_tile + CHUNK) * P)
            nc.sync.dma_start(
                out=words[(gate, operand)][:, :, cols].bitcast(I32),
                in_=dram_words[gate][operand][:, :, cols, :].rearrange("g p n t -> p g (n t)").bitcast(I32),
            )

        def load_scale_rows(gate, operand, quadrant):
            first = 32 * quadrant
            nc.sync.dma_start(
                out=planes[first : first + PLANE_ROWS * HALVES, gate, operand, :].bitcast(I32),
                in_=dram_scales[gate][operand][
                    :, PLANE_ROWS * quadrant : PLANE_ROWS * (quadrant + 1), :
                ].bitcast(I32),
            )

        def load_state(state_sb, state, first_tile=0, tiles=TILES):
            chosen = slice(first_tile, first_tile + tiles)
            nc.sync.dma_start(out=state_sb[:, chosen, :], in_=by_tile(state)[:, chosen, :])

        def load_rows(source, half):
            raw = stage.tile([P, PACK, BATCH], BF16, tag="raw", bufs=PASSES, name="raw")
            rows = source[half * K_PASS : (half + 1) * K_PASS, :]
            nc.sync.dma_start(out=raw[:], in_=rows.rearrange("(p j) b -> p j b", j=PACK))
            return raw

        def regroup(raw):
            grouped = stage.tile(
                [P, BATCH, PACK], BF16, tag="grouped", bufs=PASSES, name="grouped", align_bytes=64
            )
            for copy, cols in (
                (nc.vector.tensor_copy, slice(0, VECTOR_COLS)),
                (nc.scalar.copy, slice(VECTOR_COLS, BATCH)),
            ):
                copy(
                    out=grouped[:, cols, :].rearrange("p (c i) j -> p c j i", i=4),
                    in_=raw[:, :, cols].rearrange("p j (c i) -> p c j i", i=4),
                )
            return grouped

        def quantise(grouped, k):
            nc.vector.quantize_mx(
                out=codes[:, k, :].bitcast(FP8X4),
                scales=code_planes[:, k, :],
                in_=grouped[:].rearrange("p b j -> p (b j)"),
            )

        def mx_pass(wave, gate, tile_index, k):
            operand, half = divmod(k, HALVES)
            cols = slice(tile_index * P, (tile_index + 1) * P)
            nc.tensor.matmul_mx(
                out=wave[:],
                lhsT=words[(gate, operand)][:, half, cols].bitcast(FP8X4),
                lhsT_scale=planes[PLANE_ROWS * half : P, gate, operand, cols],
                rhs=codes[:, k, :].bitcast(FP8X4),
                rhs_scale=code_planes[:, k, :],
                start=(k == 0),
                stop=(k == PASSES - 1),
            )

        def new_wave(gate, tile_index, bank):
            return psum.tile([P, BATCH], F32, tag="bank_%d" % bank, name="wave_%d_%d" % (gate, tile_index))

        def whole_wave(gate, tile_index, bank):
            wave = new_wave(gate, tile_index, bank)
            for k in range(PASSES):
                mx_pass(wave, gate, tile_index, k)
            return wave

        def column(table, gate, tile_index):
            return table[:, TILES * gate + tile_index : TILES * gate + tile_index + 1]

        def store(dram, tile_index, result):
            nc.sync.dma_start(out=dram[tile_index * P : (tile_index + 1) * P, :], in_=result[:])

        def alternate(tiles, *stages):
            for stage_of in stages:
                for t in tiles:
                    stage_of(t)

        pairs = [(t, t + 1) for t in range(0, TILES, 2)]

        nc.vector.memset(forget_bias_row[:], 0.0)
        nc.vector.memset(bias_rows[:], 0.0)
        nc.vector.memset(warm[:], 0.0)
        nc.vector.memset(idle_rows[:], 0.0)
        nc.vector.memset(planes[:, FORGET, :, :].bitcast(I32), 0)
        nc.vector.memset(planes[:, FORGET + 1 : GATES, :, :].bitcast(I32), 0)
        nc.scalar.activation(out=warm[:], in_=warm[:], func=FUNC.Sigmoid)
        def load_bias(rows, gate):
            nc.gpsimd.dma_start(
                out=rows[TILES * gate : TILES * (gate + 1), :],
                in_=dram_bias[gate].rearrange("(t p) -> t p", p=P),
            )

        load_bias(forget_bias_row, FORGET)
        make_identity(nc, identity[:])
        for gate in (INPUT, Z, OUTPUT):
            load_bias(bias_rows, gate)
        make_identity(nc, identity_f32[:])
        x_raws = [load_rows(x, half) for half in range(HALVES)]
        for quadrant in range(QUADRANTS):
            load_scale_rows(FORGET, 0, quadrant)
        load_range(FORGET, 0, 0)
        h_raws = [load_rows(h_prev, 0)]
        h_raws.append(load_rows(h_prev, 1))
        load_range(FORGET, 0, CHUNK)
        for quadrant in range(QUADRANTS):
            load_scale_rows(FORGET, 1, quadrant)
        load_range(FORGET, 1, 0)
        load_state(m_sb, m_prev, 0, CHUNK)
        load_range(FORGET, 1, CHUNK)
        load_state(m_sb, m_prev, CHUNK, CHUNK)
        load_range(INPUT, 0, 0)
        for quadrant in range(QUADRANTS):
            load_scale_rows(INPUT, 0, quadrant)
        load_range(INPUT, 1, 0)
        for quadrant in range(QUADRANTS):
            load_scale_rows(INPUT, 1, quadrant)
        load_range(INPUT, 0, CHUNK)
        load_range(INPUT, 1, CHUNK)
        load_state(n_sb, n_prev, 0, CHUNK)
        load_state(n_sb, n_prev, CHUNK, CHUNK)
        for operand in range(2):
            for quadrant in range(QUADRANTS):
                load_scale_rows(Z, operand, quadrant)
            for half in range(HALVES):
                load_half(Z, operand, half)
        load_state(c_sb, c_prev, 0, CHUNK)
        load_state(c_sb, c_prev, CHUNK, CHUNK)
        for operand in range(2):
            for quadrant in range(QUADRANTS):
                load_scale_rows(OUTPUT, operand, quadrant)
            for half in range(HALVES):
                load_half(OUTPUT, operand, half)

        warm_up = psum.tile([P, BATCH], F32, tag="bank_%d" % (TILES - 1), name="warm_up")
        for repeat in range(WARM_UP_MATMULS):
            nc.tensor.matmul(out=warm_up[:], lhsT=idle_rows[:, 0:P], rhs=idle_rows[:], start=True, stop=True)

        forget_columns = psum.tile([P, P], BF16, tag="bank_%d" % (TILES - 2))
        nc.tensor.transpose(forget_columns[:], forget_bias_row[:], identity[:])

        x_grouped = [regroup(raw) for raw in x_raws]
        for half in range(HALVES):
            quantise(x_grouped[half], half)
        h_grouped = [regroup(raw) for raw in h_raws]
        for half in range(HALVES):
            quantise(h_grouped[half], HALVES + half)
        nc.vector.tensor_copy(out=forget_bias[:], in_=forget_columns[:, 0:TILES])
        nc.vector.tensor_scalar_add(out=bias_split[:], in0=forget_bias[:], scalar1=SPLIT)
        nc.vector.tensor_scalar_mul(out=minus_bias_split[:], in0=bias_split[:], scalar1=-1.0)

        forget_wave = [new_wave(FORGET, t, t) for t in range(CHUNK)]
        for k in range(HALVES):
            for t in range(CHUNK):
                mx_pass(forget_wave[t], FORGET, t, k)
        w_ahead = CHUNK + 2
        for t in range(CHUNK, w_ahead):
            forget_wave.append(new_wave(FORGET, t, t))
            for k in range(HALVES):
                mx_pass(forget_wave[t], FORGET, t, k)
        for t in range(CHUNK):
            for k in range(HALVES, PASSES):
                mx_pass(forget_wave[t], FORGET, t, k)
        for t in range(w_ahead, TILES):
            forget_wave.append(new_wave(FORGET, t, t))
            for k in range(HALVES):
                mx_pass(forget_wave[t], FORGET, t, k)
        for t in range(CHUNK, TILES):
            for k in range(HALVES, PASSES):
                mx_pass(forget_wave[t], FORGET, t, k)

        first = {}
        second = {}
        third = {}
        fourth = {}
        gate_o = {}
        wave = {}
        wave_o = {}

        def add_split(t):
            nc.vector.tensor_scalar_add(out=second[t][:], in0=second[t][:], scalar1=bias_split[:, t : t + 1])

        for t in range(TILES):
            first[t] = full.tile([P, BATCH], F32, tag="first", name="first_%d" % t)
            nc.scalar.activation(
                out=first[t][:], in_=forget_wave[t][:], func=FUNC.Sigmoid, bias=forget_bias[:, t : t + 1]
            )
            second[t] = full.tile([P, BATCH], F32, tag="second", name="second_%d" % t)
            nc.vector.scalar_tensor_tensor(
                out=second[t][:], in0=forget_wave[t][:], scalar=minus_bias_split[:, t : t + 1],
                in1=m_sb[:, t, :], op0=ALU.min, op1=ALU.add,
            )
            if t > 0:
                add_split(t - 1)

        add_split(TILES - 1)
        bias_columns = psum.tile([P, P], BF16, tag="bank_%d" % (CHUNK - 1))
        nc.tensor.transpose(bias_columns[:], bias_rows[:], identity[:])
        nc.vector.tensor_copy(out=bias[:], in_=bias_columns[:, 0 : GATES * TILES])
        for first_tile in range(0, TILES, CHUNK):
            chunk = range(first_tile, first_tile + CHUNK)
            for t in chunk:
                wave[t] = new_wave(INPUT, t, t)
                for k in range(HALVES):
                    mx_pass(wave[t], INPUT, t, k)
            for t in chunk:
                for k in range(HALVES, PASSES):
                    mx_pass(wave[t], INPUT, t, k)

        for t in range(TILES):
            nc.scalar.activation(out=first[t][:], in_=first[t][:], func=FUNC.Ln)
        for t in range(TILES):
            third[t] = full.tile([P, BATCH], F32, tag="third", name="third_%d" % t)
            nc.scalar.activation(out=third[t][:], in_=n_sb[:, t, :], func=FUNC.Ln, bias=1.0, scale=1.0)

        def add_log_sigmoid(t):
            nc.vector.scalar_tensor_tensor(
                out=second[t][:], in0=first[t][:], scalar=-SPLIT, in1=second[t][:],
                op0=ALU.max, op1=ALU.add,
            )

        def new_stabiliser(t):
            m_t = work.tile([P, BATCH], F32, tag="m_t", bufs=TILES)
            nc.vector.scalar_tensor_tensor(
                out=m_t[:], in0=wave[t][:], scalar=column(bias, INPUT, t), in1=second[t][:],
                op0=ALU.add, op1=ALU.max,
            )
            store(m_out, t, m_t)

        def difference(t):
            nc.vector.scalar_tensor_tensor(
                out=first[t][:], in0=wave[t][:], scalar=column(bias, INPUT, t), in1=second[t][:],
                op0=ALU.add, op1=ALU.subtract,
            )

        def positive_part(t):
            nc.vector.tensor_scalar(
                out=second[t][:], in0=first[t][:], scalar1=0.0, scalar2=EXP_CLAMP, op0=ALU.max, op1=ALU.min
            )

        def z_matmuls(t):
            wave[t] = whole_wave(Z, t, t)

        def exp_plus(t):
            nc.scalar.activation(out=first[t][:], in_=first[t][:], func=FUNC.Exp)

        def forget_factor(t):
            nc.scalar.activation(out=second[t][:], in_=second[t][:], func=FUNC.Exp, scale=-1.0)

        def inverse_n1(t):
            nc.scalar.activation(out=third[t][:], in_=third[t][:], func=FUNC.Exp, scale=-1.0)

        def tanh_z(t):
            fourth[t] = full.tile([P, BATCH], F32, tag="fourth", name="fourth_%d" % t)
            nc.scalar.activation(out=fourth[t][:], in_=wave[t][:], func=FUNC.Tanh, bias=column(bias, Z, t))

        def o_matmuls(t):
            wave_o[t] = whole_wave(OUTPUT, t, t % (TILES // 2))

        def output_gate(t):
            gate_o[t] = work.tile([P, BATCH], F32, tag="gate_o", bufs=4, name="gate_o_%d" % t)
            nc.scalar.activation(
                out=gate_o[t][:], in_=wave_o[t][:], func=FUNC.Sigmoid, bias=column(bias, OUTPUT, t)
            )

        def weigh_z(t):
            nc.vector.scalar_tensor_tensor(
                out=fourth[t][:], in0=first[t][:], scalar=math.exp(EXP_CLAMP), in1=fourth[t][:],
                op0=ALU.min, op1=ALU.mult,
            )

        def add_c(t):
            wave[t] = psum.tile([P, BATCH], F32, tag="bank_%d" % t, name="sum_%d" % t)
            nc.tensor.matmul(out=wave[t][:], lhsT=identity[:], rhs=c_sb[:, t, :], start=True, stop=False)
            nc.tensor.matmul(out=wave[t][:], lhsT=identity_f32[:], rhs=fourth[t][:], start=False, stop=True)

        def divide(t):
            nc.vector.tensor_tensor(out=first[t][:], in0=wave[t][:], in1=third[t][:], op=ALU.mult)

        def cell(t):
            nc.vector.tensor_tensor(out=fourth[t][:], in0=wave[t][:], in1=second[t][:], op=ALU.mult)
            store(c_out, t, fourth[t])

        def normaliser(t):
            nc.vector.scalar_tensor_tensor(
                out=second[t][:], in0=n_sb[:, t, :], scalar=1.0, in1=second[t][:], op0=ALU.add, op1=ALU.mult
            )
            store(n_out, t, second[t])

        def tanh_ratio(t):
            nc.scalar.activation(out=first[t][:], in_=first[t][:], func=FUNC.Tanh)

        def hidden(t):
            nc.vector.tensor_tensor(out=first[t][:], in0=first[t][:], in1=gate_o[t][:], op=ALU.mult)
            store(h_out, t, first[t])

        stages = (
            (add_log_sigmoid, new_stabiliser, difference, positive_part, z_matmuls),
            (exp_plus, tanh_z, forget_factor, inverse_n1),
            (weigh_z, add_c),
            (divide, cell, normaliser, o_matmuls),
            (tanh_ratio, output_gate),
            (hidden,),
        )
        for step in range(len(pairs) + len(stages) - 1):
            for depth, stage_steps in enumerate(stages):
                if 0 <= step - depth < len(pairs):
                    alternate(pairs[step - depth], *stage_steps)
